import numpy as np
import ml_dtypes


def mxq(x, axis, fmt="e4m3"):
    dtype, down = {"e4m3": (ml_dtypes.float8_e4m3fn, 7), "e5m2": (ml_dtypes.float8_e5m2, 14)}[fmt]
    v = np.moveaxis(np.asarray(x, np.float32).astype(ml_dtypes.bfloat16).astype(np.float64), axis, -1)
    blocks = v.reshape(v.shape[:-1] + (-1, 32))
    amax = np.abs(blocks).max(-1, keepdims=True)
    byte = np.maximum(np.where(amax > 0, np.frexp(amax)[1] - 1 + 127, 0) - down, 1)
    scale = np.exp2(byte - 127.0)
    codes = (blocks / scale).astype(np.float32).astype(dtype).astype(np.float64)
    return np.moveaxis((codes * scale).reshape(v.shape), -1, axis)


WIDE = False


def mx_kscale(k):
    if not WIDE:
        return np.ones(k)
    levels = np.array([10, -10, 5, -5, 0])
    a = np.random.permutation(np.resize(levels, k // 512 * 4)).reshape(k // 512, 4)
    idx = np.arange(k)
    return np.exp2(a[idx // 512, idx % 128 // 32])


BF16 = ml_dtypes.bfloat16


def bf(x):
    return np.asarray(x, np.float32).astype(BF16)


def f64(x):
    return np.asarray(x).astype(np.float64)


E2M1 = np.array([0.0, 0.5, 1.0, 1.5, 2.0, 3.0, 4.0, 6.0, -0.0, -0.5, -1.0, -1.5, -2.0, -3.0, -4.0, -6.0])


def pack_weight(w, fmt):
    k, n = w.shape
    w = f64(bf(w)).reshape(k // 32, 32, n)
    amax = np.abs(w).max(1)
    if fmt == "e4m3":
        byte = np.frexp(amax)[1] - 1 + 127 - 7
    else:
        mant, ex = np.frexp(amax / 6.0)
        byte = np.where(mant > 0.5, ex, ex - 1) + 127
    byte = np.clip(np.where(amax > 0, byte, 1), 1, 254)
    scaled = (w * np.exp2(127.0 - byte)[:, None, :]).reshape(k, n).astype(np.float32)
    by_word = np.ascontiguousarray(scaled.reshape(k // 512, 128, 4, n).transpose(0, 1, 3, 2))
    if fmt == "e4m3":
        words = by_word.astype(ml_dtypes.float8_e4m3fn).view(np.uint8)
    else:
        c = by_word.astype(ml_dtypes.float4_e2m1fn).view(np.uint8) & 0xF
        words = c[..., 0::2] | (c[..., 1::2] << 4)
    return np.ascontiguousarray(words), np.ascontiguousarray(byte.astype(np.uint8).reshape(k // 512, 16, n))


def unpack_weight(words, scales, fmt):
    g, p, n, _ = words.shape
    if fmt == "e4m3":
        vals = np.ascontiguousarray(words).view(ml_dtypes.float8_e4m3fn).astype(np.float64)
    else:
        nib = np.empty((g, p, n, 4), np.uint8)
        nib[..., 0::2] = words & 0xF
        nib[..., 1::2] = words >> 4
        vals = E2M1[nib]
    vals = vals * np.repeat(np.exp2(scales.astype(np.float64) - 127.0), 8, axis=1)[..., None]
    return vals.transpose(0, 1, 3, 2).reshape(g * 512, n)


B, H = 128, 2048
EPS = 1e-5
NUM_GROUPS = 4
FMT = "e4m3"


def sigmoid(v):
    return 1.0 / (1.0 + np.exp(-v))


def _group_norm(z, weight, bias):
    n, ch = z.shape
    zg = z.reshape(n, NUM_GROUPS, ch // NUM_GROUPS)
    mean = zg.mean(axis=-1, keepdims=True)
    var = zg.var(axis=-1, keepdims=True)
    zn = (zg - mean) / np.sqrt(var + EPS)
    return zn.reshape(n, ch) * weight + bias


def setup_inputs():
    s = mx_kscale(H)
    x = bf(np.random.standard_normal((1, B, H)))
    h = bf(np.random.standard_normal((B, H)) * s)
    c = bf(np.random.standard_normal((B, H)))
    w = np.random.uniform(-1.0, 1.0, (NUM_GROUPS * H, H)) / np.sqrt(H) / s[None, :]
    words, scales = pack_weight(np.ascontiguousarray(w.T), FMT)
    b = bf(np.random.standard_normal(NUM_GROUPS * H) * 0.3)
    gn_weight = bf(1.0 + 0.1 * np.random.standard_normal(NUM_GROUPS * H))
    gn_bias = bf(0.1 * np.random.standard_normal(NUM_GROUPS * H))
    return {"x": x,
            "h": h,
            "c": c,
            "W_words": words,
            "W_scales": scales,
            "b": b,
            "gn_weight": gn_weight,
            "gn_bias": gn_bias}


def reference(x, h, c, W_words, W_scales, b, gn_weight, gn_bias):
    lin = (mxq(f64(h), 1, "e4m3") @ unpack_weight(W_words, W_scales, FMT)) + f64(b)
    z = _group_norm(lin, f64(gn_weight), f64(gn_bias))
    i, f, o, g = np.split(z, NUM_GROUPS, axis=1)
    c_new = sigmoid(f) * f64(c) + sigmoid(i) * np.tanh(g)
    h_new = sigmoid(o) * np.tanh(c_new)
    return (h_new, c_new)

@@ -1,0 +1,247 @@
+from contextlib import ExitStack
+
+import concourse.mybir as mybir
+from concourse.masks import make_identity
+
+F32 = mybir.dt.float32
+BF16 = mybir.dt.bfloat16
+I32 = mybir.dt.int32
+U32 = mybir.dt.uint32
+U8 = mybir.dt.uint8
+FP8X4 = mybir.dt.float8_e4m3fn_x4
+ALU = mybir.AluOpType
+ACT = mybir.ActivationFunctionType
+AX = mybir.AxisListType
+
+P = 128
+H = 2048
+GATES = 4
+PACK = 4
+K_PASS = P * PACK
+PASSES = H // K_PASS
+N_TILE = 512
+TILES = H // N_TILE
+EPS = 1e-5
+
+ROW = 256
+ROWS_PER_VECTOR = GATES * H // ROW
+ROWS_PER_GATE = H // ROW
+ROWS_PER_BANK = N_TILE // P
+
+GATE_I, GATE_F, GATE_O, GATE_G = 0, 1, 2, 3
+GATE_ORDER = (GATE_I, GATE_G, GATE_F, GATE_O)
+
+WEIGHT_BUFS = 2 * PASSES
+LAST_PIECES = 4
+
+FLOPS = 2 * P * H * GATES * H
+
+
+def tile_lstmcell2_w_kernel(
+    tc, x, h, c, W_words, W_scales, b, gn_weight, gn_bias, out_0, out_1
+):
+    nc = tc.nc
+    with ExitStack() as stack:
+        const = stack.enter_context(tc.tile_pool(name="const", bufs=1))
+        weights = stack.enter_context(tc.tile_pool(name="weights", bufs=WEIGHT_BUFS))
+        work = stack.enter_context(tc.tile_pool(name="work", bufs=2))
+        stats = stack.enter_context(tc.tile_pool(name="stats", bufs=2))
+        setup_psum = stack.enter_context(tc.psum_pool(name="setup_psum", bufs=4))
+        acc_psum = stack.enter_context(tc.psum_pool(name="acc_psum", bufs=TILES))
+
+        vec_rows = const.tile([P, ROW], BF16)
+        nc.vector.memset(vec_rows[3 * ROWS_PER_VECTOR : P, :], 0.0)
+        for v, vector in enumerate((b, gn_weight, gn_bias)):
+            nc.sync.dma_start(
+                out=vec_rows[v * ROWS_PER_VECTOR : (v + 1) * ROWS_PER_VECTOR, :],
+                in_=vector.rearrange("(r w) -> r w", w=ROW),
+            )
+        h_sb = const.tile([P, H], BF16)
+        nc.sync.dma_start(out=h_sb[:], in_=h)
+
+        w_planes = const.tile([P, GATES * H], U8, align_bytes=64)
+        nc.vector.memset(w_planes[:].bitcast(I32), 0)
+        scales_i32 = W_scales.bitcast(I32)
+        for quadrant in range(4):
+            nc.sync.dma_start(
+                out=w_planes[32 * quadrant : 32 * quadrant + 16, :].bitcast(I32),
+                in_=scales_i32[:, 4 * quadrant : 4 * quadrant + 4, :],
+            )
+
+        ident = const.tile([P, P], F32)
+        make_identity(nc, ident[:])
+        minus_half = const.tile([P, 1], F32)
+        nc.vector.memset(minus_half[:], -0.5)
+        eps_col = const.tile([P, 1], F32)
+        nc.vector.memset(eps_col[:], EPS)
+
+        h_words = h_sb[:].bitcast(F32)
+        grouped = const.tile([P, PASSES, P, PACK], BF16, align_bytes=64)
+        grouped_words = grouped[:].bitcast(F32)
+        for pair in range(PASSES // 2):
+            h_t = setup_psum.tile([P, 2, 2, P], F32, tag="setup")
+            for g2 in range(2):
+                g = 2 * pair + g2
+                for u in range(2):
+                    nc.tensor.transpose(
+                        h_t[:, g2, u, :],
+                        h_words[:, 256 * g + u : 256 * (g + 1) : 2],
+                        ident[:],
+                    )
+            nc.vector.tensor_copy(
+                out=grouped_words[:, 2 * pair : 2 * pair + 2, :, :],
+                in_=h_t[:].rearrange("p g u m -> p g m u"),
+            )
+        h_codes = const.tile([P, PASSES * P], U32, align_bytes=64)
+        h_scales = const.tile([P, PASSES * P], U8, align_bytes=64)
+        nc.vector.quantize_mx(
+            out=h_codes[:].bitcast(FP8X4),
+            scales=h_scales[:],
+            in_=grouped[:].rearrange("p g m t -> p (g m t)"),
+        )
+
+        vec_cols_ps = setup_psum.tile([P, P], F32, tag="setup")
+        nc.tensor.transpose(vec_cols_ps[:], vec_rows[:].bitcast(F32), ident[:])
+        vec_cols = const.tile([P, P], F32)
+        nc.vector.tensor_copy(out=vec_cols[:], in_=vec_cols_ps[:])
+
+        bias_all = const.tile([P, GATES * H], BF16)
+        gain_all = const.tile([P, GATES * H], BF16)
+        shift_all = const.tile([P, GATES * H], BF16)
+        banks_done = 0
+        for gate in GATE_ORDER:
+            for v, spread_to in enumerate((bias_all, gain_all, shift_all)):
+                for part in range(ROWS_PER_GATE // ROWS_PER_BANK):
+                    first_row = gate * ROWS_PER_GATE + part * ROWS_PER_BANK
+                    spread = setup_psum.tile([P, ROWS_PER_BANK, P], F32, tag="setup")
+                    for i in range(ROWS_PER_BANK):
+                        r = v * ROWS_PER_VECTOR + first_row + i
+                        nc.tensor.transpose(
+                            spread[:, i, :], vec_cols[:, r : r + 1].to_broadcast([P, P]), ident[:]
+                        )
+                    dest = spread_to[:].bitcast(F32)[:, first_row * P : (first_row + ROWS_PER_BANK) * P]
+                    if banks_done % 2 == 0:
+                        nc.vector.tensor_copy(out=dest, in_=spread[:].rearrange("p i w -> p (i w)"))
+                    else:
+                        nc.scalar.copy(out=dest, in_=spread[:].rearrange("p i w -> p (i w)"))
+                    banks_done += 1
+
+        c_sb = const.tile([P, H], BF16)
+        words_i32 = W_words.rearrange("g p n t -> g p (n t)").bitcast(I32)
+
+        def gate_matmul(gate):
+            chunks = []
+            for g in range(PASSES):
+                chunk = weights.tile([P, H], U32, align_bytes=64)
+                nc.sync.dma_start(
+                    out=chunk[:].bitcast(I32), in_=words_i32[g, :, gate * H : (gate + 1) * H]
+                )
+                chunks.append(chunk)
+            acc = [acc_psum.tile([P, N_TILE], F32, name="acc") for t in range(TILES)]
+            for g in range(PASSES):
+                for t in range(TILES):
+                    nc.tensor.matmul_mx(
+                        out=acc[t][:],
+                        lhsT=h_codes[:, g * P : (g + 1) * P].bitcast(FP8X4),
+                        lhsT_scale=h_scales[:, g * P : (g + 1) * P],
+                        rhs=chunks[g][:, t * N_TILE : (t + 1) * N_TILE].bitcast(FP8X4),
+                        rhs_scale=w_planes[
+                            4 * g : P, gate * H + t * N_TILE : gate * H + (t + 1) * N_TILE
+                        ],
+                        start=(g == 0),
+                        stop=(g == PASSES - 1),
+                    )
+            return acc
+
+        def gate_norm(gate, acc, func, result, pieces):
+            first = gate * H
+            lin = work.tile([P, H], F32)
+            tile_sums = stats.tile([P, TILES], F32)
+            for t in range(TILES):
+                nc.vector.scalar_tensor_tensor(
+                    out=lin[:, t * N_TILE : (t + 1) * N_TILE],
+                    in0=acc[t][:],
+                    scalar=1.0,
+                    in1=bias_all[:, first + t * N_TILE : first + (t + 1) * N_TILE],
+                    op0=ALU.mult,
+                    op1=ALU.add,
+                    accum_out=tile_sums[:, t : t + 1],
+                )
+            neg_centre = stats.tile([P, 1], F32)
+            nc.vector.tensor_scalar(
+                out=neg_centre[:], in0=tile_sums[:, 0:1], scalar1=-1.0 / N_TILE, scalar2=None, op0=ALU.mult
+            )
+            squares = work.tile([P, H], BF16, bufs=1)
+            sq_sum = stats.tile([P, 1], F32)
+            nc.scalar.activation(
+                out=squares[:], in_=lin[:], func=ACT.Square, bias=neg_centre[:], scale=1.0, accum_out=sq_sum[:]
+            )
+            total = stats.tile([P, 1], F32)
+            nc.vector.tensor_reduce(out=total[:], in_=tile_sums[:], axis=AX.X, op=ALU.add)
+            neg_mean = stats.tile([P, 1], F32)
+            nc.vector.tensor_scalar(
+                out=neg_mean[:], in0=total[:], scalar1=-1.0 / H, scalar2=None, op0=ALU.mult
+            )
+            offset = stats.tile([P, 1], F32)
+            nc.vector.tensor_tensor(out=offset[:], in0=neg_centre[:], in1=neg_mean[:], op=ALU.subtract)
+            correction = stats.tile([P, 1], F32)
+            nc.vector.scalar_tensor_tensor(
+                out=correction[:], in0=offset[:], scalar=offset[:], in1=eps_col[:], op0=ALU.mult, op1=ALU.subtract
+            )
+            width = H // pieces
+            for piece in range(pieces):
+                nc.vector.scalar_tensor_tensor(
+                    out=result[:, piece * width : (piece + 1) * width],
+                    in0=lin[:, piece * width : (piece + 1) * width],
+                    scalar=neg_mean[:],
+                    in1=gain_all[:, first + piece * width : first + (piece + 1) * width],
+                    op0=ALU.add,
+                    op1=ALU.mult,
+                )
+            var_eps = stats.tile([P, 1], F32)
+            nc.vector.scalar_tensor_tensor(
+                out=var_eps[:], in0=sq_sum[:], scalar=1.0 / H, in1=correction[:], op0=ALU.mult, op1=ALU.subtract
+            )
+            rstd = stats.tile([P, 1], F32)
+            nc.gpsimd.tensor_tensor(out=rstd[:], in0=var_eps[:], in1=minus_half[:], op=ALU.pow)
+            for piece in range(pieces):
+                cols = slice(piece * width, (piece + 1) * width)
+                nc.vector.scalar_tensor_tensor(
+                    out=result[:, cols],
+                    in0=result[:, cols],
+                    scalar=rstd[:],
+                    in1=shift_all[:, first + piece * width : first + (piece + 1) * width],
+                    op0=ALU.mult,
+                    op1=ALU.add,
+                )
+                nc.scalar.activation(out=result[:, cols], in_=result[:, cols], func=func)
+
+        gate_i = const.tile([P, H], F32)
+        gate_g = const.tile([P, H], F32)
+        gate_f = const.tile([P, H], F32)
+        gate_o = const.tile([P, H], F32)
+        c_new = const.tile([P, H], F32)
+        tanh_c = const.tile([P, H], F32)
+
+        acc = gate_matmul(GATE_I)
+        nc.sync.dma_start(out=c_sb[:], in_=c)
+        gate_norm(GATE_I, acc, ACT.Sigmoid, gate_i, 1)
+
+        acc = gate_matmul(GATE_G)
+        gate_norm(GATE_G, acc, ACT.Tanh, gate_g, 1)
+        nc.vector.tensor_tensor(out=gate_i[:], in0=gate_i[:], in1=gate_g[:], op=ALU.mult)
+
+        acc = gate_matmul(GATE_F)
+        gate_norm(GATE_F, acc, ACT.Sigmoid, gate_f, 1)
+        nc.vector.tensor_tensor(out=gate_f[:], in0=gate_f[:], in1=c_sb[:], op=ALU.mult)
+        nc.vector.tensor_tensor(out=c_new[:], in0=gate_f[:], in1=gate_i[:], op=ALU.add)
+        nc.sync.dma_start(out=out_1, in_=c_new[:])
+        nc.scalar.activation(out=tanh_c[:], in_=c_new[:], func=ACT.Tanh)
+
+        acc = gate_matmul(GATE_O)
+        gate_norm(GATE_O, acc, ACT.Sigmoid, gate_o, LAST_PIECES)
+        width = H // LAST_PIECES
+        for piece in range(LAST_PIECES):
+            cols = slice(piece * width, (piece + 1) * width)
+            nc.vector.tensor_tensor(out=gate_o[:, cols], in0=gate_o[:, cols], in1=tanh_c[:, cols], op=ALU.mult)
+            nc.sync.dma_start(out=out_0[:, cols], in_=gate_o[:, cols])

@@ -27,12 +27,14 @@ ROW = 256
 ROWS_PER_VECTOR = GATES * H // ROW
 ROWS_PER_GATE = H // ROW
 ROWS_PER_BANK = N_TILE // P
+BANK_CHANNELS = ROWS_PER_BANK * ROW
+BANKS_PER_GATE = H // BANK_CHANNELS
+BIAS_ROWS, GAIN_ROWS, SHIFT_ROWS = 0, ROWS_PER_VECTOR, 2 * ROWS_PER_VECTOR
 
 GATE_I, GATE_F, GATE_O, GATE_G = 0, 1, 2, 3
 GATE_ORDER = (GATE_I, GATE_G, GATE_F, GATE_O)
 
-WEIGHT_BUFS = 2 * PASSES
-LAST_PIECES = 4
+WEIGHT_BUFS = 3 * PASSES
 
 FLOPS = 2 * P * H * GATES * H
 
@@ -42,18 +44,19 @@ def tile_lstmcell2_w_kernel(
 ):
     nc = tc.nc
     with ExitStack() as stack:
+        stack.enter_context(tc.manual_schedule())
         const = stack.enter_context(tc.tile_pool(name="const", bufs=1))
         weights = stack.enter_context(tc.tile_pool(name="weights", bufs=WEIGHT_BUFS))
         work = stack.enter_context(tc.tile_pool(name="work", bufs=2))
         stats = stack.enter_context(tc.tile_pool(name="stats", bufs=2))
-        setup_psum = stack.enter_context(tc.psum_pool(name="setup_psum", bufs=4))
+        spread_psum = stack.enter_context(tc.psum_pool(name="spread_psum", bufs=4))
         acc_psum = stack.enter_context(tc.psum_pool(name="acc_psum", bufs=TILES))
 
         vec_rows = const.tile([P, ROW], BF16)
         nc.vector.memset(vec_rows[3 * ROWS_PER_VECTOR : P, :], 0.0)
-        for v, vector in enumerate((b, gn_weight, gn_bias)):
+        for first_row, vector in ((BIAS_ROWS, b), (GAIN_ROWS, gn_weight), (SHIFT_ROWS, gn_bias)):
             nc.sync.dma_start(
-                out=vec_rows[v * ROWS_PER_VECTOR : (v + 1) * ROWS_PER_VECTOR, :],
+                out=vec_rows[first_row : first_row + ROWS_PER_VECTOR, :],
                 in_=vector.rearrange("(r w) -> r w", w=ROW),
             )
         h_sb = const.tile([P, H], BF16)
@@ -68,6 +71,19 @@ def tile_lstmcell2_w_kernel(
                 in_=scales_i32[:, 4 * quadrant : 4 * quadrant + 4, :],
             )
 
+        words_i32 = W_words.rearrange("g p n t -> g p (n t)").bitcast(I32)
+        c_sb = const.tile([P, H], BF16)
+        chunks = {}
+        for gate in GATE_ORDER:
+            for g in range(PASSES):
+                chunk = weights.tile([P, H], U32, align_bytes=64)
+                nc.sync.dma_start(
+                    out=chunk[:].bitcast(I32), in_=words_i32[g, :, gate * H : (gate + 1) * H]
+                )
+                chunks[(gate, g)] = chunk
+            if gate == GATE_ORDER[0]:
+                nc.sync.dma_start(out=c_sb[:], in_=c)
+
         ident = const.tile([P, P], F32)
         make_identity(nc, ident[:])
         minus_half = const.tile([P, 1], F32)
@@ -75,20 +91,45 @@ def tile_lstmcell2_w_kernel(
         eps_col = const.tile([P, 1], F32)
         nc.vector.memset(eps_col[:], EPS)
 
+        vec_cols_ps = spread_psum.tile([P, P], F32, tag="bank")
+        nc.tensor.transpose(vec_cols_ps[:], vec_rows[:].bitcast(F32), ident[:])
+        vec_cols = const.tile([P, P], F32)
+        nc.vector.tensor_copy(out=vec_cols[:], in_=vec_cols_ps[:])
+
+        def spread_rows(first_row):
+            bank = spread_psum.tile([P, ROWS_PER_BANK * P], F32, tag="bank")
+            for i in range(ROWS_PER_BANK):
+                nc.tensor.transpose(
+                    bank[:, i * P : (i + 1) * P],
+                    vec_cols[:, first_row + i : first_row + i + 1].to_broadcast([P, P]),
+                    ident[:],
+                )
+            return bank
+
+        def spread_gate(vector_rows, gate):
+            return [
+                spread_rows(vector_rows + gate * ROWS_PER_GATE + half * ROWS_PER_BANK)
+                for half in range(BANKS_PER_GATE)
+            ]
+
+        def channels(banks, t):
+            per_bank = BANK_CHANNELS // N_TILE
+            start = (t % per_bank) * N_TILE
+            return banks[t // per_bank][:].bitcast(BF16)[:, start : start + N_TILE]
+
         h_words = h_sb[:].bitcast(F32)
         grouped = const.tile([P, PASSES, P, PACK], BF16, align_bytes=64)
         grouped_words = grouped[:].bitcast(F32)
         for pair in range(PASSES // 2):
-            h_t = setup_psum.tile([P, 2, 2, P], F32, tag="setup")
+            h_t = spread_psum.tile([P, 2, 2, P], F32, tag="bank")
             for g2 in range(2):
                 g = 2 * pair + g2
                 for u in range(2):
                     nc.tensor.transpose(
-                        h_t[:, g2, u, :],
-                        h_words[:, 256 * g + u : 256 * (g + 1) : 2],
-                        ident[:],
+                        h_t[:, g2, u, :], h_words[:, 256 * g + u : 256 * (g + 1) : 2], ident[:]
                     )
-            nc.vector.tensor_copy(
+            copy_out = nc.vector.tensor_copy if pair == 0 else nc.scalar.copy
+            copy_out(
                 out=grouped_words[:, 2 * pair : 2 * pair + 2, :, :],
                 in_=h_t[:].rearrange("p g u m -> p g m u"),
             )
@@ -100,61 +141,35 @@ def tile_lstmcell2_w_kernel(
             in_=grouped[:].rearrange("p g m t -> p (g m t)"),
         )
 
-        vec_cols_ps = setup_psum.tile([P, P], F32, tag="setup")
-        nc.tensor.transpose(vec_cols_ps[:], vec_rows[:].bitcast(F32), ident[:])
-        vec_cols = const.tile([P, P], F32)
-        nc.vector.tensor_copy(out=vec_cols[:], in_=vec_cols_ps[:])
-
         bias_all = const.tile([P, GATES * H], BF16)
-        gain_all = const.tile([P, GATES * H], BF16)
-        shift_all = const.tile([P, GATES * H], BF16)
-        banks_done = 0
         for gate in GATE_ORDER:
-            for v, spread_to in enumerate((bias_all, gain_all, shift_all)):
-                for part in range(ROWS_PER_GATE // ROWS_PER_BANK):
-                    first_row = gate * ROWS_PER_GATE + part * ROWS_PER_BANK
-                    spread = setup_psum.tile([P, ROWS_PER_BANK, P], F32, tag="setup")
-                    for i in range(ROWS_PER_BANK):
-                        r = v * ROWS_PER_VECTOR + first_row + i
-                        nc.tensor.transpose(
-                            spread[:, i, :], vec_cols[:, r : r + 1].to_broadcast([P, P]), ident[:]
-                        )
-                    dest = spread_to[:].bitcast(F32)[:, first_row * P : (first_row + ROWS_PER_BANK) * P]
-                    if banks_done % 2 == 0:
-                        nc.vector.tensor_copy(out=dest, in_=spread[:].rearrange("p i w -> p (i w)"))
-                    else:
-                        nc.scalar.copy(out=dest, in_=spread[:].rearrange("p i w -> p (i w)"))
-                    banks_done += 1
-
-        c_sb = const.tile([P, H], BF16)
-        words_i32 = W_words.rearrange("g p n t -> g p (n t)").bitcast(I32)
+            for half, bank in enumerate(spread_gate(BIAS_ROWS, gate)):
+                first = gate * H + half * BANK_CHANNELS
+                copy_out = nc.vector.tensor_copy if half == 0 else nc.scalar.copy
+                copy_out(out=bias_all[:, first : first + BANK_CHANNELS].bitcast(F32), in_=bank[:])
 
         def gate_matmul(gate):
-            chunks = []
-            for g in range(PASSES):
-                chunk = weights.tile([P, H], U32, align_bytes=64)
-                nc.sync.dma_start(
-                    out=chunk[:].bitcast(I32), in_=words_i32[g, :, gate * H : (gate + 1) * H]
-                )
-                chunks.append(chunk)
             acc = [acc_psum.tile([P, N_TILE], F32, name="acc") for t in range(TILES)]
+            gain = None
             for g in range(PASSES):
+                if g == PASSES - 1:
+                    gain = spread_gate(GAIN_ROWS, gate)
                 for t in range(TILES):
                     nc.tensor.matmul_mx(
                         out=acc[t][:],
                         lhsT=h_codes[:, g * P : (g + 1) * P].bitcast(FP8X4),
                         lhsT_scale=h_scales[:, g * P : (g + 1) * P],
-                        rhs=chunks[g][:, t * N_TILE : (t + 1) * N_TILE].bitcast(FP8X4),
+                        rhs=chunks[(gate, g)][:, t * N_TILE : (t + 1) * N_TILE].bitcast(FP8X4),
                         rhs_scale=w_planes[
                             4 * g : P, gate * H + t * N_TILE : gate * H + (t + 1) * N_TILE
                         ],
                         start=(g == 0),
                         stop=(g == PASSES - 1),
                     )
-            return acc
+            shift = spread_gate(SHIFT_ROWS, gate)
+            return acc, gain, shift
 
-        def gate_norm(gate, acc, func, result, pieces):
-            first = gate * H
+        def gate_stats(gate, acc, gain, centred):
             lin = work.tile([P, H], F32)
             tile_sums = stats.tile([P, TILES], F32)
             for t in range(TILES):
@@ -162,7 +177,7 @@ def tile_lstmcell2_w_kernel(
                     out=lin[:, t * N_TILE : (t + 1) * N_TILE],
                     in0=acc[t][:],
                     scalar=1.0,
-                    in1=bias_all[:, first + t * N_TILE : first + (t + 1) * N_TILE],
+                    in1=bias_all[:, gate * H + t * N_TILE : gate * H + (t + 1) * N_TILE],
                     op0=ALU.mult,
                     op1=ALU.add,
                     accum_out=tile_sums[:, t : t + 1],
@@ -188,13 +203,12 @@ def tile_lstmcell2_w_kernel(
             nc.vector.scalar_tensor_tensor(
                 out=correction[:], in0=offset[:], scalar=offset[:], in1=eps_col[:], op0=ALU.mult, op1=ALU.subtract
             )
-            width = H // pieces
-            for piece in range(pieces):
+            for t in range(TILES):
                 nc.vector.scalar_tensor_tensor(
-                    out=result[:, piece * width : (piece + 1) * width],
-                    in0=lin[:, piece * width : (piece + 1) * width],
+                    out=centred[:, t * N_TILE : (t + 1) * N_TILE],
+                    in0=lin[:, t * N_TILE : (t + 1) * N_TILE],
                     scalar=neg_mean[:],
-                    in1=gain_all[:, first + piece * width : first + (piece + 1) * width],
+                    in1=channels(gain, t),
                     op0=ALU.add,
                     op1=ALU.mult,
                 )
@@ -204,17 +218,19 @@ def tile_lstmcell2_w_kernel(
             )
             rstd = stats.tile([P, 1], F32)
             nc.gpsimd.tensor_tensor(out=rstd[:], in0=var_eps[:], in1=minus_half[:], op=ALU.pow)
-            for piece in range(pieces):
-                cols = slice(piece * width, (piece + 1) * width)
-                nc.vector.scalar_tensor_tensor(
-                    out=result[:, cols],
-                    in0=result[:, cols],
-                    scalar=rstd[:],
-                    in1=shift_all[:, first + piece * width : first + (piece + 1) * width],
-                    op0=ALU.mult,
-                    op1=ALU.add,
-                )
-                nc.scalar.activation(out=result[:, cols], in_=result[:, cols], func=func)
+            return rstd
+
+        def gate_tile(centred, rstd, shift, func, t):
+            cols = slice(t * N_TILE, (t + 1) * N_TILE)
+            nc.vector.scalar_tensor_tensor(
+                out=centred[:, cols],
+                in0=centred[:, cols],
+                scalar=rstd[:],
+                in1=channels(shift, t),
+                op0=ALU.mult,
+                op1=ALU.add,
+            )
+            nc.scalar.activation(out=centred[:, cols], in_=centred[:, cols], func=func)
 
         gate_i = const.tile([P, H], F32)
         gate_g = const.tile([P, H], F32)
@@ -223,25 +239,36 @@ def tile_lstmcell2_w_kernel(
         c_new = const.tile([P, H], F32)
         tanh_c = const.tile([P, H], F32)
 
-        acc = gate_matmul(GATE_I)
-        nc.sync.dma_start(out=c_sb[:], in_=c)
-        gate_norm(GATE_I, acc, ACT.Sigmoid, gate_i, 1)
+        acc, gain, shift = gate_matmul(GATE_I)
+        rstd = gate_stats(GATE_I, acc, gain, gate_i)
+        for t in range(TILES):
+            gate_tile(gate_i, rstd, shift, ACT.Sigmoid, t)
 
-        acc = gate_matmul(GATE_G)
-        gate_norm(GATE_G, acc, ACT.Tanh, gate_g, 1)
-        nc.vector.tensor_tensor(out=gate_i[:], in0=gate_i[:], in1=gate_g[:], op=ALU.mult)
+        acc, gain, shift = gate_matmul(GATE_G)
+        rstd = gate_stats(GATE_G, acc, gain, gate_g)
+        for t in range(TILES):
+            cols = slice(t * N_TILE, (t + 1) * N_TILE)
+            gate_tile(gate_g, rstd, shift, ACT.Tanh, t)
+            nc.gpsimd.tensor_tensor(out=gate_i[:, cols], in0=gate_i[:, cols], in1=gate_g[:, cols], op=ALU.mult)
 
-        acc = gate_matmul(GATE_F)
-        gate_norm(GATE_F, acc, ACT.Sigmoid, gate_f, 1)
-        nc.vector.tensor_tensor(out=gate_f[:], in0=gate_f[:], in1=c_sb[:], op=ALU.mult)
-        nc.vector.tensor_tensor(out=c_new[:], in0=gate_f[:], in1=gate_i[:], op=ALU.add)
+        acc, gain, shift = gate_matmul(GATE_F)
+        rstd = gate_stats(GATE_F, acc, gain, gate_f)
+        for t in range(TILES):
+            cols = slice(t * N_TILE, (t + 1) * N_TILE)
+            gate_tile(gate_f, rstd, shift, ACT.Sigmoid, t)
+            nc.gpsimd.tensor_tensor(out=gate_f[:, cols], in0=gate_f[:, cols], in1=c_sb[:, cols], op=ALU.mult)
+            nc.gpsimd.tensor_tensor(out=c_new[:, cols], in0=gate_f[:, cols], in1=gate_i[:, cols], op=ALU.add)
         nc.sync.dma_start(out=out_1, in_=c_new[:])
-        nc.scalar.activation(out=tanh_c[:], in_=c_new[:], func=ACT.Tanh)
 
-        acc = gate_matmul(GATE_O)
-        gate_norm(GATE_O, acc, ACT.Sigmoid, gate_o, LAST_PIECES)
-        width = H // LAST_PIECES
-        for piece in range(LAST_PIECES):
-            cols = slice(piece * width, (piece + 1) * width)
-            nc.vector.tensor_tensor(out=gate_o[:, cols], in0=gate_o[:, cols], in1=tanh_c[:, cols], op=ALU.mult)
-            nc.sync.dma_start(out=out_0[:, cols], in_=gate_o[:, cols])
+        acc, gain, shift = gate_matmul(GATE_O)
+        rstd = gate_stats(GATE_O, acc, gain, gate_o)
+        for t in range(TILES):
+            cols = slice(t * N_TILE, (t + 1) * N_TILE)
+            nc.scalar.activation(out=tanh_c[:, cols], in_=c_new[:, cols], func=ACT.Tanh)
+        for t in range(TILES + 1):
+            if t < TILES:
+                gate_tile(gate_o, rstd, shift, ACT.Sigmoid, t)
+            if t > 0:
+                cols = slice((t - 1) * N_TILE, t * N_TILE)
+                nc.vector.tensor_tensor(out=gate_o[:, cols], in0=gate_o[:, cols], in1=tanh_c[:, cols], op=ALU.mult)
+                nc.sync.dma_start(out=out_0[:, cols], in_=gate_o[:, cols])

@@ -73,16 +73,27 @@ def tile_lstmcell2_w_kernel(
 
         words_i32 = W_words.rearrange("g p n t -> g p (n t)").bitcast(I32)
         c_sb = const.tile([P, H], BF16)
-        chunks = {}
-        for gate in GATE_ORDER:
+        w_words = {}
+        for gate in GATE_ORDER[:-1]:
             for g in range(PASSES):
-                chunk = weights.tile([P, H], U32, align_bytes=64)
+                chunk = weights.tile([P, TILES, N_TILE], U32, align_bytes=64)
                 nc.sync.dma_start(
-                    out=chunk[:].bitcast(I32), in_=words_i32[g, :, gate * H : (gate + 1) * H]
+                    out=chunk[:].rearrange("p t n -> p (t n)").bitcast(I32),
+                    in_=words_i32[g, :, gate * H : (gate + 1) * H],
                 )
-                chunks[(gate, g)] = chunk
+                for t in range(TILES):
+                    w_words[(gate, g, t)] = chunk[:, t, :]
             if gate == GATE_ORDER[0]:
                 nc.sync.dma_start(out=c_sb[:], in_=c)
+        for t in range(TILES):
+            first = GATE_ORDER[-1] * H + t * N_TILE
+            chunk = weights.tile([P, PASSES, N_TILE], U32, align_bytes=64)
+            nc.sync.dma_start(
+                out=chunk[:].bitcast(I32),
+                in_=words_i32[:, :, first : first + N_TILE].rearrange("g p n -> p g n"),
+            )
+            for g in range(PASSES):
+                w_words[(GATE_ORDER[-1], g, t)] = chunk[:, g, :]
 
         ident = const.tile([P, P], F32)
         make_identity(nc, ident[:])
@@ -148,33 +159,37 @@ def tile_lstmcell2_w_kernel(
                 copy_out = nc.vector.tensor_copy if half == 0 else nc.scalar.copy
                 copy_out(out=bias_all[:, first : first + BANK_CHANNELS].bitcast(F32), in_=bank[:])
 
-        def gate_matmul(gate):
+        def gate_matmul(gate, steps):
             acc = [acc_psum.tile([P, N_TILE], F32, name="acc") for t in range(TILES)]
             gain = None
-            for g in range(PASSES):
-                if g == PASSES - 1:
+            for index, (g, t) in enumerate(steps):
+                if index == len(steps) - TILES:
                     gain = spread_gate(GAIN_ROWS, gate)
-                for t in range(TILES):
-                    nc.tensor.matmul_mx(
-                        out=acc[t][:],
-                        lhsT=h_codes[:, g * P : (g + 1) * P].bitcast(FP8X4),
-                        lhsT_scale=h_scales[:, g * P : (g + 1) * P],
-                        rhs=chunks[(gate, g)][:, t * N_TILE : (t + 1) * N_TILE].bitcast(FP8X4),
-                        rhs_scale=w_planes[
-                            4 * g : P, gate * H + t * N_TILE : gate * H + (t + 1) * N_TILE
-                        ],
-                        start=(g == 0),
-                        stop=(g == PASSES - 1),
-                    )
+                nc.tensor.matmul_mx(
+                    out=acc[t][:],
+                    lhsT=h_codes[:, g * P : (g + 1) * P].bitcast(FP8X4),
+                    lhsT_scale=h_scales[:, g * P : (g + 1) * P],
+                    rhs=w_words[(gate, g, t)].bitcast(FP8X4),
+                    rhs_scale=w_planes[4 * g : P, gate * H + t * N_TILE : gate * H + (t + 1) * N_TILE],
+                    start=(g == 0),
+                    stop=(g == PASSES - 1),
+                )
             shift = spread_gate(SHIFT_ROWS, gate)
             return acc, gain, shift
 
+        by_pass = [(g, t) for g in range(PASSES) for t in range(TILES)]
+        by_tile = [(g, t) for t in range(TILES) for g in range(PASSES)]
+
         def gate_stats(gate, acc, gain, centred):
             lin = work.tile([P, H], F32)
+            squares = work.tile([P, N_TILE], BF16)
             tile_sums = stats.tile([P, TILES], F32)
+            tile_sq_sums = stats.tile([P, TILES], F32)
+            neg_centre = stats.tile([P, 1], F32)
             for t in range(TILES):
+                cols = slice(t * N_TILE, (t + 1) * N_TILE)
                 nc.vector.scalar_tensor_tensor(
-                    out=lin[:, t * N_TILE : (t + 1) * N_TILE],
+                    out=lin[:, cols],
                     in0=acc[t][:],
                     scalar=1.0,
                     in1=bias_all[:, gate * H + t * N_TILE : gate * H + (t + 1) * N_TILE],
@@ -182,15 +197,14 @@ def tile_lstmcell2_w_kernel(
                     op1=ALU.add,
                     accum_out=tile_sums[:, t : t + 1],
                 )
-            neg_centre = stats.tile([P, 1], F32)
-            nc.vector.tensor_scalar(
-                out=neg_centre[:], in0=tile_sums[:, 0:1], scalar1=-1.0 / N_TILE, scalar2=None, op0=ALU.mult
-            )
-            squares = work.tile([P, H], BF16, bufs=1)
-            sq_sum = stats.tile([P, 1], F32)
-            nc.scalar.activation(
-                out=squares[:], in_=lin[:], func=ACT.Square, bias=neg_centre[:], scale=1.0, accum_out=sq_sum[:]
-            )
+                if t == 0:
+                    nc.vector.tensor_scalar(
+                        out=neg_centre[:], in0=tile_sums[:, 0:1], scalar1=-1.0 / N_TILE, scalar2=None, op0=ALU.mult
+                    )
+                nc.scalar.activation(
+                    out=squares[:], in_=lin[:, cols], func=ACT.Square, bias=neg_centre[:], scale=1.0,
+                    accum_out=tile_sq_sums[:, t : t + 1],
+                )
             total = stats.tile([P, 1], F32)
             nc.vector.tensor_reduce(out=total[:], in_=tile_sums[:], axis=AX.X, op=ALU.add)
             neg_mean = stats.tile([P, 1], F32)
@@ -203,6 +217,14 @@ def tile_lstmcell2_w_kernel(
             nc.vector.scalar_tensor_tensor(
                 out=correction[:], in0=offset[:], scalar=offset[:], in1=eps_col[:], op0=ALU.mult, op1=ALU.subtract
             )
+            sq_sum = stats.tile([P, 1], F32)
+            nc.vector.tensor_reduce(out=sq_sum[:], in_=tile_sq_sums[:], axis=AX.X, op=ALU.add)
+            var_eps = stats.tile([P, 1], F32)
+            nc.vector.scalar_tensor_tensor(
+                out=var_eps[:], in0=sq_sum[:], scalar=1.0 / H, in1=correction[:], op0=ALU.mult, op1=ALU.subtract
+            )
+            rstd = stats.tile([P, 1], F32)
+            nc.gpsimd.tensor_tensor(out=rstd[:], in0=var_eps[:], in1=minus_half[:], op=ALU.pow)
             for t in range(TILES):
                 nc.vector.scalar_tensor_tensor(
                     out=centred[:, t * N_TILE : (t + 1) * N_TILE],
@@ -212,12 +234,6 @@ def tile_lstmcell2_w_kernel(
                     op0=ALU.add,
                     op1=ALU.mult,
                 )
-            var_eps = stats.tile([P, 1], F32)
-            nc.vector.scalar_tensor_tensor(
-                out=var_eps[:], in0=sq_sum[:], scalar=1.0 / H, in1=correction[:], op0=ALU.mult, op1=ALU.subtract
-            )
-            rstd = stats.tile([P, 1], F32)
-            nc.gpsimd.tensor_tensor(out=rstd[:], in0=var_eps[:], in1=minus_half[:], op=ALU.pow)
             return rstd
 
         def gate_tile(centred, rstd, shift, func, t):
@@ -239,36 +255,35 @@ def tile_lstmcell2_w_kernel(
         c_new = const.tile([P, H], F32)
         tanh_c = const.tile([P, H], F32)
 
-        acc, gain, shift = gate_matmul(GATE_I)
+        acc, gain, shift = gate_matmul(GATE_I, by_pass)
         rstd = gate_stats(GATE_I, acc, gain, gate_i)
         for t in range(TILES):
             gate_tile(gate_i, rstd, shift, ACT.Sigmoid, t)
 
-        acc, gain, shift = gate_matmul(GATE_G)
+        acc, gain, shift = gate_matmul(GATE_G, by_pass)
         rstd = gate_stats(GATE_G, acc, gain, gate_g)
         for t in range(TILES):
             cols = slice(t * N_TILE, (t + 1) * N_TILE)
             gate_tile(gate_g, rstd, shift, ACT.Tanh, t)
             nc.gpsimd.tensor_tensor(out=gate_i[:, cols], in0=gate_i[:, cols], in1=gate_g[:, cols], op=ALU.mult)
 
-        acc, gain, shift = gate_matmul(GATE_F)
+        acc, gain, shift = gate_matmul(GATE_F, by_pass)
         rstd = gate_stats(GATE_F, acc, gain, gate_f)
         for t in range(TILES):
             cols = slice(t * N_TILE, (t + 1) * N_TILE)
             gate_tile(gate_f, rstd, shift, ACT.Sigmoid, t)
             nc.gpsimd.tensor_tensor(out=gate_f[:, cols], in0=gate_f[:, cols], in1=c_sb[:, cols], op=ALU.mult)
-            nc.gpsimd.tensor_tensor(out=c_new[:, cols], in0=gate_f[:, cols], in1=gate_i[:, cols], op=ALU.add)
-        nc.sync.dma_start(out=out_1, in_=c_new[:])
 
-        acc, gain, shift = gate_matmul(GATE_O)
+        acc, gain, shift = gate_matmul(GATE_O, by_tile)
         rstd = gate_stats(GATE_O, acc, gain, gate_o)
         for t in range(TILES):
+            gate_tile(gate_o, rstd, shift, ACT.Sigmoid, t)
+        for t in range(TILES):
             cols = slice(t * N_TILE, (t + 1) * N_TILE)
+            nc.gpsimd.tensor_tensor(out=c_new[:, cols], in0=gate_f[:, cols], in1=gate_i[:, cols], op=ALU.add)
+            nc.sync.dma_start(out=out_1[:, cols], in_=c_new[:, cols])
             nc.scalar.activation(out=tanh_c[:, cols], in_=c_new[:, cols], func=ACT.Tanh)
-        for t in range(TILES + 1):
-            if t < TILES:
-                gate_tile(gate_o, rstd, shift, ACT.Sigmoid, t)
-            if t > 0:
-                cols = slice((t - 1) * N_TILE, t * N_TILE)
-                nc.vector.tensor_tensor(out=gate_o[:, cols], in0=gate_o[:, cols], in1=tanh_c[:, cols], op=ALU.mult)
-                nc.sync.dma_start(out=out_0[:, cols], in_=gate_o[:, cols])
+        for t in range(TILES):
+            cols = slice(t * N_TILE, (t + 1) * N_TILE)
+            nc.vector.tensor_tensor(out=gate_o[:, cols], in0=gate_o[:, cols], in1=tanh_c[:, cols], op=ALU.mult)
+            nc.sync.dma_start(out=out_0[:, cols], in_=gate_o[:, cols])

@@ -55,7 +55,7 @@ def tile_lstmcell2_w_kernel(
         vec_rows = const.tile([P, ROW], BF16)
         nc.vector.memset(vec_rows[3 * ROWS_PER_VECTOR : P, :], 0.0)
         for first_row, vector in ((BIAS_ROWS, b), (GAIN_ROWS, gn_weight), (SHIFT_ROWS, gn_bias)):
-            nc.sync.dma_start(
+            nc.scalar.dma_start(
                 out=vec_rows[first_row : first_row + ROWS_PER_VECTOR, :],
                 in_=vector.rearrange("(r w) -> r w", w=ROW),
             )
@@ -64,11 +64,11 @@ def tile_lstmcell2_w_kernel(
 
         w_planes = const.tile([P, GATES * H], U8, align_bytes=64)
         nc.vector.memset(w_planes[:].bitcast(I32), 0)
-        scales_i32 = W_scales.bitcast(I32)
+        scale_words = W_scales.bitcast(F32)
         for quadrant in range(4):
-            nc.sync.dma_start(
-                out=w_planes[32 * quadrant : 32 * quadrant + 16, :].bitcast(I32),
-                in_=scales_i32[:, 4 * quadrant : 4 * quadrant + 4, :],
+            nc.scalar.dma_start(
+                out=w_planes[32 * quadrant : 32 * quadrant + 16, :].bitcast(F32),
+                in_=scale_words[:, 4 * quadrant : 4 * quadrant + 4, :],
             )
 
         words_i32 = W_words.rearrange("g p n t -> g p (n t)").bitcast(I32)

@@ -55,7 +55,7 @@ def tile_lstmcell2_w_kernel(
         vec_rows = const.tile([P, ROW], BF16)
         nc.vector.memset(vec_rows[3 * ROWS_PER_VECTOR : P, :], 0.0)
         for first_row, vector in ((BIAS_ROWS, b), (GAIN_ROWS, gn_weight), (SHIFT_ROWS, gn_bias)):
-            nc.scalar.dma_start(
+            nc.sync.dma_start(
                 out=vec_rows[first_row : first_row + ROWS_PER_VECTOR, :],
                 in_=vector.rearrange("(r w) -> r w", w=ROW),
             )
@@ -64,11 +64,11 @@ def tile_lstmcell2_w_kernel(
 
         w_planes = const.tile([P, GATES * H], U8, align_bytes=64)
         nc.vector.memset(w_planes[:].bitcast(I32), 0)
-        scale_words = W_scales.bitcast(F32)
+        scales_i32 = W_scales.bitcast(I32)
         for quadrant in range(4):
-            nc.scalar.dma_start(
-                out=w_planes[32 * quadrant : 32 * quadrant + 16, :].bitcast(F32),
-                in_=scale_words[:, 4 * quadrant : 4 * quadrant + 4, :],
+            nc.sync.dma_start(
+                out=w_planes[32 * quadrant : 32 * quadrant + 16, :].bitcast(I32),
+                in_=scales_i32[:, 4 * quadrant : 4 * quadrant + 4, :],
             )
 
         words_i32 = W_words.rearrange("g p n t -> g p (n t)").bitcast(I32)
@@ -122,11 +122,6 @@ def tile_lstmcell2_w_kernel(
                 spread_rows(vector_rows + gate * ROWS_PER_GATE + half * ROWS_PER_BANK)
                 for half in range(BANKS_PER_GATE)
             ]
-
-        def channels(banks, t):
-            per_bank = BANK_CHANNELS // N_TILE
-            start = (t % per_bank) * N_TILE
-            return banks[t // per_bank][:].bitcast(BF16)[:, start : start + N_TILE]
 
         h_words = h_sb[:].bitcast(F32)
         grouped = const.tile([P, PASSES, P, PACK], BF16, align_bytes=64)
@@ -198,9 +193,7 @@ def tile_lstmcell2_w_kernel(
                     accum_out=tile_sums[:, t : t + 1],
                 )
                 if t == 0:
-                    nc.vector.tensor_scalar(
-                        out=neg_centre[:], in0=tile_sums[:, 0:1], scalar1=-1.0 / N_TILE, scalar2=None, op0=ALU.mult
-                    )
+                    nc.scalar.mul(out=neg_centre[:], in_=tile_sums[:, 0:1], mul=-1.0 / N_TILE)
                 nc.scalar.activation(
                     out=squares[:], in_=lin[:, cols], func=ACT.Square, bias=neg_centre[:], scale=1.0,
                     accum_out=tile_sq_sums[:, t : t + 1],
@@ -211,38 +204,43 @@ def tile_lstmcell2_w_kernel(
             nc.vector.tensor_scalar(
                 out=neg_mean[:], in0=total[:], scalar1=-1.0 / H, scalar2=None, op0=ALU.mult
             )
-            offset = stats.tile([P, 1], F32)
-            nc.vector.tensor_tensor(out=offset[:], in0=neg_centre[:], in1=neg_mean[:], op=ALU.subtract)
-            correction = stats.tile([P, 1], F32)
-            nc.vector.scalar_tensor_tensor(
-                out=correction[:], in0=offset[:], scalar=offset[:], in1=eps_col[:], op0=ALU.mult, op1=ALU.subtract
-            )
-            sq_sum = stats.tile([P, 1], F32)
-            nc.vector.tensor_reduce(out=sq_sum[:], in_=tile_sq_sums[:], axis=AX.X, op=ALU.add)
-            var_eps = stats.tile([P, 1], F32)
-            nc.vector.scalar_tensor_tensor(
-                out=var_eps[:], in0=sq_sum[:], scalar=1.0 / H, in1=correction[:], op0=ALU.mult, op1=ALU.subtract
-            )
-            rstd = stats.tile([P, 1], F32)
-            nc.gpsimd.tensor_tensor(out=rstd[:], in0=var_eps[:], in1=minus_half[:], op=ALU.pow)
-            for t in range(TILES):
+            for half in range(BANKS_PER_GATE):
+                cols = slice(half * BANK_CHANNELS, (half + 1) * BANK_CHANNELS)
                 nc.vector.scalar_tensor_tensor(
-                    out=centred[:, t * N_TILE : (t + 1) * N_TILE],
-                    in0=lin[:, t * N_TILE : (t + 1) * N_TILE],
+                    out=centred[:, cols],
+                    in0=lin[:, cols],
                     scalar=neg_mean[:],
-                    in1=channels(gain, t),
+                    in1=gain[half][:].bitcast(BF16),
                     op0=ALU.add,
                     op1=ALU.mult,
                 )
+            copied = stats.tile([P, TILES], F32)
+            sq_sum = stats.tile([P, 1], F32)
+            nc.scalar.activation(out=copied[:], in_=tile_sq_sums[:], func=ACT.Identity, accum_out=sq_sum[:])
+            offset_sq = stats.tile([P, 1], F32)
+            nc.scalar.activation(
+                out=offset_sq[:], in_=neg_mean[:], func=ACT.Square, bias=neg_centre[:], scale=-1.0
+            )
+            eps_less = stats.tile([P, 1], F32)
+            nc.scalar.activation(
+                out=eps_less[:], in_=offset_sq[:], func=ACT.Identity, bias=eps_col[:], scale=-1.0
+            )
+            var_eps = stats.tile([P, 1], F32)
+            nc.scalar.activation(
+                out=var_eps[:], in_=sq_sum[:], func=ACT.Identity, bias=eps_less[:], scale=1.0 / H
+            )
+            rstd = stats.tile([P, 1], F32)
+            nc.gpsimd.tensor_tensor(out=rstd[:], in0=var_eps[:], in1=minus_half[:], op=ALU.pow)
             return rstd
 
-        def gate_tile(centred, rstd, shift, func, t):
-            cols = slice(t * N_TILE, (t + 1) * N_TILE)
+        def gate_piece(centred, rstd, shift, func, first, width):
+            cols = slice(first, first + width)
+            in_bank = first % BANK_CHANNELS
             nc.vector.scalar_tensor_tensor(
                 out=centred[:, cols],
                 in0=centred[:, cols],
                 scalar=rstd[:],
-                in1=channels(shift, t),
+                in1=shift[first // BANK_CHANNELS][:].bitcast(BF16)[:, in_bank : in_bank + width],
                 op0=ALU.mult,
                 op1=ALU.add,
             )
@@ -257,33 +255,33 @@ def tile_lstmcell2_w_kernel(
 
         acc, gain, shift = gate_matmul(GATE_I, by_pass)
         rstd = gate_stats(GATE_I, acc, gain, gate_i)
-        for t in range(TILES):
-            gate_tile(gate_i, rstd, shift, ACT.Sigmoid, t)
+        for first in range(0, H, BANK_CHANNELS):
+            gate_piece(gate_i, rstd, shift, ACT.Sigmoid, first, BANK_CHANNELS)
 
         acc, gain, shift = gate_matmul(GATE_G, by_pass)
         rstd = gate_stats(GATE_G, acc, gain, gate_g)
-        for t in range(TILES):
-            cols = slice(t * N_TILE, (t + 1) * N_TILE)
-            gate_tile(gate_g, rstd, shift, ACT.Tanh, t)
+        for first in range(0, H, BANK_CHANNELS):
+            cols = slice(first, first + BANK_CHANNELS)
+            gate_piece(gate_g, rstd, shift, ACT.Tanh, first, BANK_CHANNELS)
             nc.gpsimd.tensor_tensor(out=gate_i[:, cols], in0=gate_i[:, cols], in1=gate_g[:, cols], op=ALU.mult)
 
         acc, gain, shift = gate_matmul(GATE_F, by_pass)
         rstd = gate_stats(GATE_F, acc, gain, gate_f)
-        for t in range(TILES):
-            cols = slice(t * N_TILE, (t + 1) * N_TILE)
-            gate_tile(gate_f, rstd, shift, ACT.Sigmoid, t)
+        for first in range(0, H, BANK_CHANNELS):
+            cols = slice(first, first + BANK_CHANNELS)
+            gate_piece(gate_f, rstd, shift, ACT.Sigmoid, first, BANK_CHANNELS)
             nc.gpsimd.tensor_tensor(out=gate_f[:, cols], in0=gate_f[:, cols], in1=c_sb[:, cols], op=ALU.mult)
 
         acc, gain, shift = gate_matmul(GATE_O, by_tile)
         rstd = gate_stats(GATE_O, acc, gain, gate_o)
-        for t in range(TILES):
-            gate_tile(gate_o, rstd, shift, ACT.Sigmoid, t)
-        for t in range(TILES):
-            cols = slice(t * N_TILE, (t + 1) * N_TILE)
+        for first in range(0, H, N_TILE):
+            gate_piece(gate_o, rstd, shift, ACT.Sigmoid, first, N_TILE)
+        for first in range(0, H, N_TILE):
+            cols = slice(first, first + N_TILE)
             nc.gpsimd.tensor_tensor(out=c_new[:, cols], in0=gate_f[:, cols], in1=gate_i[:, cols], op=ALU.add)
             nc.sync.dma_start(out=out_1[:, cols], in_=c_new[:, cols])
             nc.scalar.activation(out=tanh_c[:, cols], in_=c_new[:, cols], func=ACT.Tanh)
-        for t in range(TILES):
-            cols = slice(t * N_TILE, (t + 1) * N_TILE)
+        for first in range(0, H, N_TILE):
+            cols = slice(first, first + N_TILE)
             nc.vector.tensor_tensor(out=gate_o[:, cols], in0=gate_o[:, cols], in1=tanh_c[:, cols], op=ALU.mult)
             nc.sync.dma_start(out=out_0[:, cols], in_=gate_o[:, cols])

@@ -47,10 +47,21 @@ def tile_lstmcell2_w_kernel(
         stack.enter_context(tc.manual_schedule())
         const = stack.enter_context(tc.tile_pool(name="const", bufs=1))
         weights = stack.enter_context(tc.tile_pool(name="weights", bufs=WEIGHT_BUFS))
+        ends = stack.enter_context(tc.tile_pool(name="ends", bufs=2))
         work = stack.enter_context(tc.tile_pool(name="work", bufs=2))
         stats = stack.enter_context(tc.tile_pool(name="stats", bufs=2))
         spread_psum = stack.enter_context(tc.psum_pool(name="spread_psum", bufs=4))
         acc_psum = stack.enter_context(tc.psum_pool(name="acc_psum", bufs=TILES))
+
+        w_planes = const.tile([P, GATES * H], U8, align_bytes=64)
+        scales_i32 = W_scales.bitcast(I32)
+        for gate in GATE_ORDER:
+            nc.vector.memset(w_planes[:, gate * H : (gate + 1) * H].bitcast(I32), 0)
+            for quadrant in range(4):
+                nc.sync.dma_start(
+                    out=w_planes[32 * quadrant : 32 * quadrant + 16, gate * H : (gate + 1) * H].bitcast(I32),
+                    in_=scales_i32[:, 4 * quadrant : 4 * quadrant + 4, gate * H // 4 : (gate + 1) * H // 4],
+                )
 
         vec_rows = const.tile([P, ROW], BF16)
         nc.vector.memset(vec_rows[3 * ROWS_PER_VECTOR : P, :], 0.0)
@@ -62,38 +73,47 @@ def tile_lstmcell2_w_kernel(
         h_sb = const.tile([P, H], BF16)
         nc.sync.dma_start(out=h_sb[:], in_=h)
 
-        w_planes = const.tile([P, GATES * H], U8, align_bytes=64)
-        nc.vector.memset(w_planes[:].bitcast(I32), 0)
-        scales_i32 = W_scales.bitcast(I32)
-        for quadrant in range(4):
-            nc.sync.dma_start(
-                out=w_planes[32 * quadrant : 32 * quadrant + 16, :].bitcast(I32),
-                in_=scales_i32[:, 4 * quadrant : 4 * quadrant + 4, :],
-            )
-
         words_i32 = W_words.rearrange("g p n t -> g p (n t)").bitcast(I32)
         c_sb = const.tile([P, H], BF16)
         w_words = {}
-        for gate in GATE_ORDER[:-1]:
-            for g in range(PASSES):
-                chunk = weights.tile([P, TILES, N_TILE], U32, align_bytes=64)
-                nc.sync.dma_start(
-                    out=chunk[:].rearrange("p t n -> p (t n)").bitcast(I32),
-                    in_=words_i32[g, :, gate * H : (gate + 1) * H],
-                )
-                for t in range(TILES):
-                    w_words[(gate, g, t)] = chunk[:, t, :]
-            if gate == GATE_ORDER[0]:
-                nc.sync.dma_start(out=c_sb[:], in_=c)
-        for t in range(TILES):
-            first = GATE_ORDER[-1] * H + t * N_TILE
-            chunk = weights.tile([P, PASSES, N_TILE], U32, align_bytes=64)
+
+        def load_pass(gate, g):
+            chunk = weights.tile([P, TILES, N_TILE], U32, align_bytes=64)
+            nc.sync.dma_start(
+                out=chunk[:].rearrange("p t n -> p (t n)").bitcast(I32),
+                in_=words_i32[g, :, gate * H : (gate + 1) * H],
+            )
+            for t in range(TILES):
+                w_words[(gate, g, t)] = chunk[:, t, :]
+
+        for g in range(PASSES):
+            load_pass(GATE_ORDER[0], g)
+        nc.sync.dma_start(out=c_sb[:], in_=c)
+        for gate in GATE_ORDER[1:]:
+            for g in range(2):
+                load_pass(gate, g)
+            chunk = weights.tile([P, 2, 2 * N_TILE], U32, align_bytes=64)
             nc.sync.dma_start(
                 out=chunk[:].bitcast(I32),
-                in_=words_i32[:, :, first : first + N_TILE].rearrange("g p n -> p g n"),
+                in_=words_i32[2:4, :, gate * H : gate * H + 2 * N_TILE].rearrange("g p n -> p g n"),
             )
-            for g in range(PASSES):
-                w_words[(GATE_ORDER[-1], g, t)] = chunk[:, g, :]
+            for g in (2, 3):
+                for t in (0, 1):
+                    w_words[(gate, g, t)] = chunk[:, g - 2, t * N_TILE : (t + 1) * N_TILE]
+            half_pass = ends.tile([P, 2 * N_TILE], U32, align_bytes=64)
+            nc.sync.dma_start(
+                out=half_pass[:].bitcast(I32),
+                in_=words_i32[2, :, gate * H + 2 * N_TILE : (gate + 1) * H],
+            )
+            for t in (2, 3):
+                w_words[(gate, 2, t)] = half_pass[:, (t - 2) * N_TILE : (t - 1) * N_TILE]
+            for t in (2, 3):
+                piece = ends.tile([P, N_TILE], U32, align_bytes=64, name="piece%d" % t)
+                nc.sync.dma_start(
+                    out=piece[:].bitcast(I32),
+                    in_=words_i32[3, :, gate * H + t * N_TILE : gate * H + (t + 1) * N_TILE],
+                )
+                w_words[(gate, 3, t)] = piece[:]
 
         ident = const.tile([P, P], F32)
         make_identity(nc, ident[:])
@@ -154,11 +174,11 @@ def tile_lstmcell2_w_kernel(
                 copy_out = nc.vector.tensor_copy if half == 0 else nc.scalar.copy
                 copy_out(out=bias_all[:, first : first + BANK_CHANNELS].bitcast(F32), in_=bank[:])
 
-        def gate_matmul(gate, steps):
+        def gate_matmul(gate, steps, before_gain):
             acc = [acc_psum.tile([P, N_TILE], F32, name="acc") for t in range(TILES)]
             gain = None
             for index, (g, t) in enumerate(steps):
-                if index == len(steps) - TILES:
+                if index == len(steps) - before_gain:
                     gain = spread_gate(GAIN_ROWS, gate)
                 nc.tensor.matmul_mx(
                     out=acc[t][:],
@@ -173,9 +193,13 @@ def tile_lstmcell2_w_kernel(
             return acc, gain, shift
 
         by_pass = [(g, t) for g in range(PASSES) for t in range(TILES)]
-        by_tile = [(g, t) for t in range(TILES) for g in range(PASSES)]
+        tiles_at_the_end = (
+            [(g, t) for g in (0, 1) for t in range(TILES)]
+            + [(g, t) for t in (0, 1) for g in (2, 3)]
+            + [(2, 2), (2, 3), (3, 2), (3, 3)]
+        )
 
-        def gate_stats(gate, acc, gain, centred):
+        def gate_centred(gate, acc, gain, centred):
             lin = work.tile([P, H], F32)
             squares = work.tile([P, N_TILE], BF16)
             tile_sums = stats.tile([P, TILES], F32)
@@ -229,11 +253,14 @@ def tile_lstmcell2_w_kernel(
             nc.scalar.activation(
                 out=var_eps[:], in_=sq_sum[:], func=ACT.Identity, bias=eps_less[:], scale=1.0 / H
             )
+            return var_eps
+
+        def inverse_root(var_eps):
             rstd = stats.tile([P, 1], F32)
             nc.gpsimd.tensor_tensor(out=rstd[:], in0=var_eps[:], in1=minus_half[:], op=ALU.pow)
             return rstd
 
-        def gate_piece(centred, rstd, shift, func, first, width):
+        def scale_and_shift(centred, rstd, shift, first, width):
             cols = slice(first, first + width)
             in_bank = first % BANK_CHANNELS
             nc.vector.scalar_tensor_tensor(
@@ -244,7 +271,9 @@ def tile_lstmcell2_w_kernel(
                 op0=ALU.mult,
                 op1=ALU.add,
             )
-            nc.scalar.activation(out=centred[:, cols], in_=centred[:, cols], func=func)
+
+        def squash(tile, func, first, width):
+            nc.scalar.activation(out=tile[:, first : first + width], in_=tile[:, first : first + width], func=func)
 
         gate_i = const.tile([P, H], F32)
         gate_g = const.tile([P, H], F32)
@@ -253,34 +282,54 @@ def tile_lstmcell2_w_kernel(
         c_new = const.tile([P, H], F32)
         tanh_c = const.tile([P, H], F32)
 
-        acc, gain, shift = gate_matmul(GATE_I, by_pass)
-        rstd = gate_stats(GATE_I, acc, gain, gate_i)
+        acc, gain, shift = gate_matmul(GATE_I, by_pass, TILES)
+        rstd = inverse_root(gate_centred(GATE_I, acc, gain, gate_i))
         for first in range(0, H, BANK_CHANNELS):
-            gate_piece(gate_i, rstd, shift, ACT.Sigmoid, first, BANK_CHANNELS)
+            scale_and_shift(gate_i, rstd, shift, first, BANK_CHANNELS)
+            squash(gate_i, ACT.Sigmoid, first, BANK_CHANNELS)
 
-        acc, gain, shift = gate_matmul(GATE_G, by_pass)
-        rstd = gate_stats(GATE_G, acc, gain, gate_g)
+        acc, gain, shift = gate_matmul(GATE_G, tiles_at_the_end, TILES)
+        rstd = inverse_root(gate_centred(GATE_G, acc, gain, gate_g))
         for first in range(0, H, BANK_CHANNELS):
             cols = slice(first, first + BANK_CHANNELS)
-            gate_piece(gate_g, rstd, shift, ACT.Tanh, first, BANK_CHANNELS)
+            scale_and_shift(gate_g, rstd, shift, first, BANK_CHANNELS)
+            squash(gate_g, ACT.Tanh, first, BANK_CHANNELS)
             nc.gpsimd.tensor_tensor(out=gate_i[:, cols], in0=gate_i[:, cols], in1=gate_g[:, cols], op=ALU.mult)
 
-        acc, gain, shift = gate_matmul(GATE_F, by_pass)
-        rstd = gate_stats(GATE_F, acc, gain, gate_f)
-        for first in range(0, H, BANK_CHANNELS):
-            cols = slice(first, first + BANK_CHANNELS)
-            gate_piece(gate_f, rstd, shift, ACT.Sigmoid, first, BANK_CHANNELS)
+        acc, gain, shift = gate_matmul(GATE_F, tiles_at_the_end, TILES)
+        rstd = inverse_root(gate_centred(GATE_F, acc, gain, gate_f))
+        for first in range(0, H, N_TILE):
+            cols = slice(first, first + N_TILE)
+            scale_and_shift(gate_f, rstd, shift, first, N_TILE)
+            squash(gate_f, ACT.Sigmoid, first, N_TILE)
             nc.gpsimd.tensor_tensor(out=gate_f[:, cols], in0=gate_f[:, cols], in1=c_sb[:, cols], op=ALU.mult)
 
-        acc, gain, shift = gate_matmul(GATE_O, by_tile)
-        rstd = gate_stats(GATE_O, acc, gain, gate_o)
-        for first in range(0, H, N_TILE):
-            gate_piece(gate_o, rstd, shift, ACT.Sigmoid, first, N_TILE)
-        for first in range(0, H, N_TILE):
+        def new_cell(first):
             cols = slice(first, first + N_TILE)
             nc.gpsimd.tensor_tensor(out=c_new[:, cols], in0=gate_f[:, cols], in1=gate_i[:, cols], op=ALU.add)
             nc.sync.dma_start(out=out_1[:, cols], in_=c_new[:, cols])
+
+        def tanh_cell(first):
+            cols = slice(first, first + N_TILE)
             nc.scalar.activation(out=tanh_c[:, cols], in_=c_new[:, cols], func=ACT.Tanh)
+
+        acc, gain, shift = gate_matmul(GATE_O, tiles_at_the_end, TILES)
+        var_eps = gate_centred(GATE_O, acc, gain, gate_o)
+        new_cell(0 * N_TILE)
+        rstd = inverse_root(var_eps)
+        new_cell(1 * N_TILE)
+        new_cell(2 * N_TILE)
+        new_cell(3 * N_TILE)
+        for first in range(0, H, N_TILE):
+            scale_and_shift(gate_o, rstd, shift, first, N_TILE)
+        tanh_cell(0 * N_TILE)
+        squash(gate_o, ACT.Sigmoid, 0 * N_TILE, N_TILE)
+        tanh_cell(1 * N_TILE)
+        squash(gate_o, ACT.Sigmoid, 1 * N_TILE, N_TILE)
+        squash(gate_o, ACT.Sigmoid, 2 * N_TILE, N_TILE)
+        tanh_cell(2 * N_TILE)
+        squash(gate_o, ACT.Sigmoid, 3 * N_TILE, N_TILE)
+        tanh_cell(3 * N_TILE)
         for first in range(0, H, N_TILE):
             cols = slice(first, first + N_TILE)
             nc.vector.tensor_tensor(out=gate_o[:, cols], in0=gate_o[:, cols], in1=tanh_c[:, cols], op=ALU.mult)

@@ -36,6 +36,9 @@ GATE_ORDER = (GATE_I, GATE_G, GATE_F, GATE_O)
 
 WEIGHT_BUFS = 3 * PASSES
 
+SMALL_FIRST = ((0, 256), (256, 256), (512, 512), (1024, 512), (1536, 512))
+SMALL_LAST = ((0, 512), (512, 512), (1024, 512), (1536, 256), (1792, 256))
+
 FLOPS = 2 * P * H * GATES * H
 
 
@@ -100,27 +103,21 @@ def tile_lstmcell2_w_kernel(
             for g in (2, 3):
                 for t in (0, 1):
                     w_words[(gate, g, t)] = chunk[:, g - 2, t * N_TILE : (t + 1) * N_TILE]
-            half_pass = ends.tile([P, 2 * N_TILE], U32, align_bytes=64)
-            nc.sync.dma_start(
-                out=half_pass[:].bitcast(I32),
-                in_=words_i32[2, :, gate * H + 2 * N_TILE : (gate + 1) * H],
-            )
             for t in (2, 3):
-                w_words[(gate, 2, t)] = half_pass[:, (t - 2) * N_TILE : (t - 1) * N_TILE]
-            for t in (2, 3):
-                piece = ends.tile([P, N_TILE], U32, align_bytes=64, name="piece%d" % t)
-                nc.sync.dma_start(
-                    out=piece[:].bitcast(I32),
-                    in_=words_i32[3, :, gate * H + t * N_TILE : gate * H + (t + 1) * N_TILE],
-                )
-                w_words[(gate, 3, t)] = piece[:]
+                for g in (2, 3):
+                    piece = ends.tile([P, N_TILE], U32, align_bytes=64, name="piece%d%d" % (g, t))
+                    nc.sync.dma_start(
+                        out=piece[:].bitcast(I32),
+                        in_=words_i32[g, :, gate * H + t * N_TILE : gate * H + (t + 1) * N_TILE],
+                    )
+                    w_words[(gate, g, t)] = piece[:]
 
         ident = const.tile([P, P], F32)
         make_identity(nc, ident[:])
         minus_half = const.tile([P, 1], F32)
         nc.vector.memset(minus_half[:], -0.5)
-        eps_col = const.tile([P, 1], F32)
-        nc.vector.memset(eps_col[:], EPS)
+        eps_share = const.tile([P, 1], F32)
+        nc.vector.memset(eps_share[:], EPS / (TILES - 1))
 
         vec_cols_ps = spread_psum.tile([P, P], F32, tag="bank")
         nc.tensor.transpose(vec_cols_ps[:], vec_rows[:].bitcast(F32), ident[:])
@@ -196,7 +193,7 @@ def tile_lstmcell2_w_kernel(
         tiles_at_the_end = (
             [(g, t) for g in (0, 1) for t in range(TILES)]
             + [(g, t) for t in (0, 1) for g in (2, 3)]
-            + [(2, 2), (2, 3), (3, 2), (3, 3)]
+            + [(g, t) for t in (2, 3) for g in (2, 3)]
         )
 
         def gate_centred(gate, acc, gain, centred):
@@ -205,6 +202,9 @@ def tile_lstmcell2_w_kernel(
             tile_sums = stats.tile([P, TILES], F32)
             tile_sq_sums = stats.tile([P, TILES], F32)
             neg_centre = stats.tile([P, 1], F32)
+            early_sum = stats.tile([P, 1], F32)
+            early_sq = stats.tile([P, 1], F32)
+            copied = stats.tile([P, TILES - 1], F32)
             for t in range(TILES):
                 cols = slice(t * N_TILE, (t + 1) * N_TILE)
                 nc.vector.scalar_tensor_tensor(
@@ -222,11 +222,16 @@ def tile_lstmcell2_w_kernel(
                     out=squares[:], in_=lin[:, cols], func=ACT.Square, bias=neg_centre[:], scale=1.0,
                     accum_out=tile_sq_sums[:, t : t + 1],
                 )
-            total = stats.tile([P, 1], F32)
-            nc.vector.tensor_reduce(out=total[:], in_=tile_sums[:], axis=AX.X, op=ALU.add)
+                if t == TILES - 2:
+                    nc.vector.tensor_reduce(out=early_sum[:], in_=tile_sums[:, 0 : TILES - 1], axis=AX.X, op=ALU.add)
+                    nc.scalar.activation(
+                        out=copied[:], in_=tile_sq_sums[:, 0 : TILES - 1], func=ACT.Identity,
+                        bias=eps_share[:], scale=1.0 / H, accum_out=early_sq[:],
+                    )
             neg_mean = stats.tile([P, 1], F32)
             nc.vector.tensor_scalar(
-                out=neg_mean[:], in0=total[:], scalar1=-1.0 / H, scalar2=None, op0=ALU.mult
+                out=neg_mean[:], in0=tile_sums[:, TILES - 1 : TILES], scalar1=early_sum[:], scalar2=-1.0 / H,
+                op0=ALU.add, op1=ALU.mult,
             )
             for half in range(BANKS_PER_GATE):
                 cols = slice(half * BANK_CHANNELS, (half + 1) * BANK_CHANNELS)
@@ -238,20 +243,18 @@ def tile_lstmcell2_w_kernel(
                     op0=ALU.add,
                     op1=ALU.mult,
                 )
-            copied = stats.tile([P, TILES], F32)
-            sq_sum = stats.tile([P, 1], F32)
-            nc.scalar.activation(out=copied[:], in_=tile_sq_sums[:], func=ACT.Identity, accum_out=sq_sum[:])
             offset_sq = stats.tile([P, 1], F32)
             nc.scalar.activation(
                 out=offset_sq[:], in_=neg_mean[:], func=ACT.Square, bias=neg_centre[:], scale=-1.0
             )
-            eps_less = stats.tile([P, 1], F32)
+            early_less = stats.tile([P, 1], F32)
             nc.scalar.activation(
-                out=eps_less[:], in_=offset_sq[:], func=ACT.Identity, bias=eps_col[:], scale=-1.0
+                out=early_less[:], in_=offset_sq[:], func=ACT.Identity, bias=early_sq[:], scale=-1.0
             )
             var_eps = stats.tile([P, 1], F32)
             nc.scalar.activation(
-                out=var_eps[:], in_=sq_sum[:], func=ACT.Identity, bias=eps_less[:], scale=1.0 / H
+                out=var_eps[:], in_=tile_sq_sums[:, TILES - 1 : TILES], func=ACT.Identity, bias=early_less[:],
+                scale=1.0 / H,
             )
             return var_eps
 
@@ -298,39 +301,43 @@ def tile_lstmcell2_w_kernel(
 
         acc, gain, shift = gate_matmul(GATE_F, tiles_at_the_end, TILES)
         rstd = inverse_root(gate_centred(GATE_F, acc, gain, gate_f))
-        for first in range(0, H, N_TILE):
-            cols = slice(first, first + N_TILE)
-            scale_and_shift(gate_f, rstd, shift, first, N_TILE)
-            squash(gate_f, ACT.Sigmoid, first, N_TILE)
+        for first, width in SMALL_FIRST:
+            cols = slice(first, first + width)
+            scale_and_shift(gate_f, rstd, shift, first, width)
+            squash(gate_f, ACT.Sigmoid, first, width)
             nc.gpsimd.tensor_tensor(out=gate_f[:, cols], in0=gate_f[:, cols], in1=c_sb[:, cols], op=ALU.mult)
 
-        def new_cell(first):
-            cols = slice(first, first + N_TILE)
+        def new_cell(piece):
+            cols = slice(piece[0], piece[0] + piece[1])
             nc.gpsimd.tensor_tensor(out=c_new[:, cols], in0=gate_f[:, cols], in1=gate_i[:, cols], op=ALU.add)
             nc.sync.dma_start(out=out_1[:, cols], in_=c_new[:, cols])
 
-        def tanh_cell(first):
-            cols = slice(first, first + N_TILE)
+        def tanh_cell(piece):
+            cols = slice(piece[0], piece[0] + piece[1])
             nc.scalar.activation(out=tanh_c[:, cols], in_=c_new[:, cols], func=ACT.Tanh)
+
+        def sigmoid_o(piece):
+            squash(gate_o, ACT.Sigmoid, piece[0], piece[1])
 
         acc, gain, shift = gate_matmul(GATE_O, tiles_at_the_end, TILES)
         var_eps = gate_centred(GATE_O, acc, gain, gate_o)
-        new_cell(0 * N_TILE)
+        new_cell(SMALL_LAST[0])
         rstd = inverse_root(var_eps)
-        new_cell(1 * N_TILE)
-        new_cell(2 * N_TILE)
-        new_cell(3 * N_TILE)
-        for first in range(0, H, N_TILE):
-            scale_and_shift(gate_o, rstd, shift, first, N_TILE)
-        tanh_cell(0 * N_TILE)
-        squash(gate_o, ACT.Sigmoid, 0 * N_TILE, N_TILE)
-        tanh_cell(1 * N_TILE)
-        squash(gate_o, ACT.Sigmoid, 1 * N_TILE, N_TILE)
-        squash(gate_o, ACT.Sigmoid, 2 * N_TILE, N_TILE)
-        tanh_cell(2 * N_TILE)
-        squash(gate_o, ACT.Sigmoid, 3 * N_TILE, N_TILE)
-        tanh_cell(3 * N_TILE)
-        for first in range(0, H, N_TILE):
-            cols = slice(first, first + N_TILE)
+        for piece in SMALL_LAST[1:]:
+            new_cell(piece)
+        for first, width in SMALL_LAST:
+            scale_and_shift(gate_o, rstd, shift, first, width)
+        tanh_cell(SMALL_LAST[0])
+        sigmoid_o(SMALL_LAST[0])
+        tanh_cell(SMALL_LAST[1])
+        sigmoid_o(SMALL_LAST[1])
+        sigmoid_o(SMALL_LAST[2])
+        tanh_cell(SMALL_LAST[2])
+        sigmoid_o(SMALL_LAST[3])
+        sigmoid_o(SMALL_LAST[4])
+        tanh_cell(SMALL_LAST[3])
+        tanh_cell(SMALL_LAST[4])
+        for first, width in SMALL_LAST:
+            cols = slice(first, first + width)
             nc.vector.tensor_tensor(out=gate_o[:, cols], in0=gate_o[:, cols], in1=tanh_c[:, cols], op=ALU.mult)
             nc.sync.dma_start(out=out_0[:, cols], in_=gate_o[:, cols])

@@ -37,7 +37,7 @@ GATE_ORDER = (GATE_I, GATE_G, GATE_F, GATE_O)
 WEIGHT_BUFS = 3 * PASSES
 
 SMALL_FIRST = ((0, 256), (256, 256), (512, 512), (1024, 512), (1536, 512))
-SMALL_LAST = ((0, 512), (512, 512), (1024, 512), (1536, 256), (1792, 256))
+EQUAL = ((0, 512), (512, 512), (1024, 512), (1536, 512))
 
 FLOPS = 2 * P * H * GATES * H
 
@@ -103,14 +103,20 @@ def tile_lstmcell2_w_kernel(
             for g in (2, 3):
                 for t in (0, 1):
                     w_words[(gate, g, t)] = chunk[:, g - 2, t * N_TILE : (t + 1) * N_TILE]
+            half_pass = ends.tile([P, 2 * N_TILE], U32, align_bytes=64)
+            nc.sync.dma_start(
+                out=half_pass[:].bitcast(I32),
+                in_=words_i32[2, :, gate * H + 2 * N_TILE : (gate + 1) * H],
+            )
             for t in (2, 3):
-                for g in (2, 3):
-                    piece = ends.tile([P, N_TILE], U32, align_bytes=64, name="piece%d%d" % (g, t))
-                    nc.sync.dma_start(
-                        out=piece[:].bitcast(I32),
-                        in_=words_i32[g, :, gate * H + t * N_TILE : gate * H + (t + 1) * N_TILE],
-                    )
-                    w_words[(gate, g, t)] = piece[:]
+                w_words[(gate, 2, t)] = half_pass[:, (t - 2) * N_TILE : (t - 1) * N_TILE]
+            for t in (2, 3):
+                piece = ends.tile([P, N_TILE], U32, align_bytes=64, name="piece%d" % t)
+                nc.sync.dma_start(
+                    out=piece[:].bitcast(I32),
+                    in_=words_i32[3, :, gate * H + t * N_TILE : gate * H + (t + 1) * N_TILE],
+                )
+                w_words[(gate, 3, t)] = piece[:]
 
         ident = const.tile([P, P], F32)
         make_identity(nc, ident[:])
@@ -193,7 +199,7 @@ def tile_lstmcell2_w_kernel(
         tiles_at_the_end = (
             [(g, t) for g in (0, 1) for t in range(TILES)]
             + [(g, t) for t in (0, 1) for g in (2, 3)]
-            + [(g, t) for t in (2, 3) for g in (2, 3)]
+            + [(2, 2), (2, 3), (3, 2), (3, 3)]
         )
 
         def gate_centred(gate, acc, gain, centred):
@@ -321,23 +327,21 @@ def tile_lstmcell2_w_kernel(
 
         acc, gain, shift = gate_matmul(GATE_O, tiles_at_the_end, TILES)
         var_eps = gate_centred(GATE_O, acc, gain, gate_o)
-        new_cell(SMALL_LAST[0])
+        new_cell(EQUAL[0])
         rstd = inverse_root(var_eps)
-        for piece in SMALL_LAST[1:]:
+        for piece in EQUAL[1:]:
             new_cell(piece)
-        for first, width in SMALL_LAST:
+        for first, width in EQUAL:
             scale_and_shift(gate_o, rstd, shift, first, width)
-        tanh_cell(SMALL_LAST[0])
-        sigmoid_o(SMALL_LAST[0])
-        tanh_cell(SMALL_LAST[1])
-        sigmoid_o(SMALL_LAST[1])
-        sigmoid_o(SMALL_LAST[2])
-        tanh_cell(SMALL_LAST[2])
-        sigmoid_o(SMALL_LAST[3])
-        sigmoid_o(SMALL_LAST[4])
-        tanh_cell(SMALL_LAST[3])
-        tanh_cell(SMALL_LAST[4])
-        for first, width in SMALL_LAST:
+        tanh_cell(EQUAL[0])
+        sigmoid_o(EQUAL[0])
+        tanh_cell(EQUAL[1])
+        sigmoid_o(EQUAL[1])
+        sigmoid_o(EQUAL[2])
+        tanh_cell(EQUAL[2])
+        sigmoid_o(EQUAL[3])
+        tanh_cell(EQUAL[3])
+        for first, width in EQUAL:
             cols = slice(first, first + width)
             nc.vector.tensor_tensor(out=gate_o[:, cols], in0=gate_o[:, cols], in1=tanh_c[:, cols], op=ALU.mult)
             nc.sync.dma_start(out=out_0[:, cols], in_=gate_o[:, cols])

@@ -56,6 +56,9 @@ def tile_lstmcell2_w_kernel(
         spread_psum = stack.enter_context(tc.psum_pool(name="spread_psum", bufs=4))
         acc_psum = stack.enter_context(tc.psum_pool(name="acc_psum", bufs=TILES))
 
+        h_sb = const.tile([P, H], BF16)
+        nc.sync.dma_start(out=h_sb[:], in_=h)
+
         w_planes = const.tile([P, GATES * H], U8, align_bytes=64)
         scales_i32 = W_scales.bitcast(I32)
         for gate in GATE_ORDER:
@@ -73,8 +76,6 @@ def tile_lstmcell2_w_kernel(
                 out=vec_rows[first_row : first_row + ROWS_PER_VECTOR, :],
                 in_=vector.rearrange("(r w) -> r w", w=ROW),
             )
-        h_sb = const.tile([P, H], BF16)
-        nc.sync.dma_start(out=h_sb[:], in_=h)
 
         words_i32 = W_words.rearrange("g p n t -> g p (n t)").bitcast(I32)
         c_sb = const.tile([P, H], BF16)

@@ -93,17 +93,24 @@ def tile_lstmcell2_w_kernel(
         for g in range(PASSES):
             load_pass(GATE_ORDER[0], g)
         nc.sync.dma_start(out=c_sb[:], in_=c)
-        for gate in GATE_ORDER[1:]:
-            for g in range(2):
-                load_pass(gate, g)
+        def load_two_tiles(gate, first_tile):
             chunk = weights.tile([P, 2, 2 * N_TILE], U32, align_bytes=64)
+            first = gate * H + first_tile * N_TILE
             nc.sync.dma_start(
                 out=chunk[:].bitcast(I32),
-                in_=words_i32[2:4, :, gate * H : gate * H + 2 * N_TILE].rearrange("g p n -> p g n"),
+                in_=words_i32[2:4, :, first : first + 2 * N_TILE].rearrange("g p n -> p g n"),
             )
             for g in (2, 3):
                 for t in (0, 1):
-                    w_words[(gate, g, t)] = chunk[:, g - 2, t * N_TILE : (t + 1) * N_TILE]
+                    w_words[(gate, g, first_tile + t)] = chunk[:, g - 2, t * N_TILE : (t + 1) * N_TILE]
+
+        for gate in GATE_ORDER[1:]:
+            for g in range(2):
+                load_pass(gate, g)
+            load_two_tiles(gate, 0)
+            if gate == GATE_ORDER[1]:
+                load_two_tiles(gate, 2)
+                continue
             half_pass = ends.tile([P, 2 * N_TILE], U32, align_bytes=64)
             nc.sync.dma_start(
                 out=half_pass[:].bitcast(I32),
@@ -197,6 +204,9 @@ def tile_lstmcell2_w_kernel(
             return acc, gain, shift
 
         by_pass = [(g, t) for g in range(PASSES) for t in range(TILES)]
+        two_tiles_at_the_end = [(g, t) for g in (0, 1) for t in range(TILES)] + [
+            (g, t) for t in range(TILES) for g in (2, 3)
+        ]
         tiles_at_the_end = (
             [(g, t) for g in (0, 1) for t in range(TILES)]
             + [(g, t) for t in (0, 1) for g in (2, 3)]
@@ -298,7 +308,7 @@ def tile_lstmcell2_w_kernel(
             scale_and_shift(gate_i, rstd, shift, first, BANK_CHANNELS)
             squash(gate_i, ACT.Sigmoid, first, BANK_CHANNELS)
 
-        acc, gain, shift = gate_matmul(GATE_G, tiles_at_the_end, TILES)
+        acc, gain, shift = gate_matmul(GATE_G, two_tiles_at_the_end, TILES)
         rstd = inverse_root(gate_centred(GATE_G, acc, gain, gate_g))
         for first in range(0, H, BANK_CHANNELS):
             cols = slice(first, first + BANK_CHANNELS)
@@ -317,11 +327,11 @@ def tile_lstmcell2_w_kernel(
         def new_cell(piece):
             cols = slice(piece[0], piece[0] + piece[1])
             nc.gpsimd.tensor_tensor(out=c_new[:, cols], in0=gate_f[:, cols], in1=gate_i[:, cols], op=ALU.add)
-            nc.sync.dma_start(out=out_1[:, cols], in_=c_new[:, cols])
 
         def tanh_cell(piece):
             cols = slice(piece[0], piece[0] + piece[1])
             nc.scalar.activation(out=tanh_c[:, cols], in_=c_new[:, cols], func=ACT.Tanh)
+            nc.scalar.dma_start(out=out_1[:, cols], in_=c_new[:, cols])
 
         def sigmoid_o(piece):
             squash(gate_o, ACT.Sigmoid, piece[0], piece[1])

@@ -108,7 +108,7 @@ def tile_lstmcell2_w_kernel(
             for g in range(2):
                 load_pass(gate, g)
             load_two_tiles(gate, 0)
-            if gate == GATE_ORDER[1]:
+            if gate != GATE_ORDER[-1]:
                 load_two_tiles(gate, 2)
                 continue
             half_pass = ends.tile([P, 2 * N_TILE], U32, align_bytes=64)
@@ -316,7 +316,7 @@ def tile_lstmcell2_w_kernel(
             squash(gate_g, ACT.Tanh, first, BANK_CHANNELS)
             nc.gpsimd.tensor_tensor(out=gate_i[:, cols], in0=gate_i[:, cols], in1=gate_g[:, cols], op=ALU.mult)
 
-        acc, gain, shift = gate_matmul(GATE_F, tiles_at_the_end, TILES)
+        acc, gain, shift = gate_matmul(GATE_F, two_tiles_at_the_end, TILES)
         rstd = inverse_root(gate_centred(GATE_F, acc, gain, gate_f))
         for first, width in SMALL_FIRST:
             cols = slice(first, first + width)
@@ -324,35 +324,52 @@ def tile_lstmcell2_w_kernel(
             squash(gate_f, ACT.Sigmoid, first, width)
             nc.gpsimd.tensor_tensor(out=gate_f[:, cols], in0=gate_f[:, cols], in1=c_sb[:, cols], op=ALU.mult)
 
-        def new_cell(piece):
-            cols = slice(piece[0], piece[0] + piece[1])
+        def new_cell(first, width):
+            cols = slice(first, first + width)
             nc.gpsimd.tensor_tensor(out=c_new[:, cols], in0=gate_f[:, cols], in1=gate_i[:, cols], op=ALU.add)
 
-        def tanh_cell(piece):
-            cols = slice(piece[0], piece[0] + piece[1])
+        def tanh_cell(first, width):
+            cols = slice(first, first + width)
             nc.scalar.activation(out=tanh_c[:, cols], in_=c_new[:, cols], func=ACT.Tanh)
+
+        def store_cell(tile_first):
+            cols = slice(tile_first, tile_first + N_TILE)
             nc.scalar.dma_start(out=out_1[:, cols], in_=c_new[:, cols])
 
         def sigmoid_o(piece):
             squash(gate_o, ACT.Sigmoid, piece[0], piece[1])
 
-        acc, gain, shift = gate_matmul(GATE_O, tiles_at_the_end, TILES)
-        var_eps = gate_centred(GATE_O, acc, gain, gate_o)
-        new_cell(EQUAL[0])
-        rstd = inverse_root(var_eps)
-        for piece in EQUAL[1:]:
-            new_cell(piece)
-        for first, width in EQUAL:
-            scale_and_shift(gate_o, rstd, shift, first, width)
-        tanh_cell(EQUAL[0])
-        sigmoid_o(EQUAL[0])
-        tanh_cell(EQUAL[1])
-        sigmoid_o(EQUAL[1])
-        sigmoid_o(EQUAL[2])
-        tanh_cell(EQUAL[2])
-        sigmoid_o(EQUAL[3])
-        tanh_cell(EQUAL[3])
-        for first, width in EQUAL:
+        def output(first, width):
             cols = slice(first, first + width)
             nc.vector.tensor_tensor(out=gate_o[:, cols], in0=gate_o[:, cols], in1=tanh_c[:, cols], op=ALU.mult)
-            nc.sync.dma_start(out=out_0[:, cols], in_=gate_o[:, cols])
+
+        acc, gain, shift = gate_matmul(GATE_O, tiles_at_the_end, TILES)
+        var_eps = gate_centred(GATE_O, acc, gain, gate_o)
+        halves = ((3 * N_TILE, N_TILE // 2), (3 * N_TILE + N_TILE // 2, N_TILE // 2))
+        new_cell(0, N_TILE)
+        rstd = inverse_root(var_eps)
+        new_cell(N_TILE, N_TILE)
+        new_cell(2 * N_TILE, N_TILE)
+        for first, width in halves:
+            new_cell(first, width)
+        for first, width in EQUAL:
+            scale_and_shift(gate_o, rstd, shift, first, width)
+        tanh_cell(0, N_TILE)
+        store_cell(0)
+        sigmoid_o(EQUAL[0])
+        tanh_cell(N_TILE, N_TILE)
+        store_cell(N_TILE)
+        sigmoid_o(EQUAL[1])
+        sigmoid_o(EQUAL[2])
+        tanh_cell(2 * N_TILE, N_TILE)
+        store_cell(2 * N_TILE)
+        sigmoid_o(EQUAL[3])
+        for first, width in halves:
+            tanh_cell(first, width)
+        store_cell(3 * N_TILE)
+        for first, width in EQUAL[:3]:
+            output(first, width)
+            nc.sync.dma_start(out=out_0[:, first : first + width], in_=gate_o[:, first : first + width])
+        for first, width in halves:
+            output(first, width)
+        nc.sync.dma_start(out=out_0[:, 3 * N_TILE : H], in_=gate_o[:, 3 * N_TILE : H])

@@ -343,7 +343,7 @@ def tile_lstmcell2_w_kernel(
             cols = slice(first, first + width)
             nc.vector.tensor_tensor(out=gate_o[:, cols], in0=gate_o[:, cols], in1=tanh_c[:, cols], op=ALU.mult)
 
-        acc, gain, shift = gate_matmul(GATE_O, tiles_at_the_end, TILES)
+        acc, gain, shift = gate_matmul(GATE_O, tiles_at_the_end, 2 * TILES)
         var_eps = gate_centred(GATE_O, acc, gain, gate_o)
         halves = ((3 * N_TILE, N_TILE // 2), (3 * N_TILE + N_TILE // 2, N_TILE // 2))
         new_cell(0, N_TILE)

@@ -60,13 +60,14 @@ def tile_lstmcell2_w_kernel(
         nc.sync.dma_start(out=h_sb[:], in_=h)
 
         w_planes = const.tile([P, GATES * H], U8, align_bytes=64)
-        scales_i32 = W_scales.bitcast(I32)
-        for gate in GATE_ORDER:
-            nc.vector.memset(w_planes[:, gate * H : (gate + 1) * H].bitcast(I32), 0)
+        ident = const.tile([P, P], F32)
+        make_identity(nc, ident[:])
+        for first, width, queue, words in ((0, H, nc.sync, I32), (H, 3 * H, nc.gpsimd, F32)):
+            nc.vector.memset(w_planes[:, first : first + width].bitcast(I32), 0)
             for quadrant in range(4):
-                nc.sync.dma_start(
-                    out=w_planes[32 * quadrant : 32 * quadrant + 16, gate * H : (gate + 1) * H].bitcast(I32),
-                    in_=scales_i32[:, 4 * quadrant : 4 * quadrant + 4, gate * H // 4 : (gate + 1) * H // 4],
+                queue.dma_start(
+                    out=w_planes[32 * quadrant : 32 * quadrant + 16, first : first + width].bitcast(words),
+                    in_=W_scales.bitcast(words)[:, 4 * quadrant : 4 * quadrant + 4, first // 4 : (first + width) // 4],
                 )
 
         vec_rows = const.tile([P, ROW], BF16)
@@ -126,8 +127,6 @@ def tile_lstmcell2_w_kernel(
                 )
                 w_words[(gate, 3, t)] = piece[:]
 
-        ident = const.tile([P, P], F32)
-        make_identity(nc, ident[:])
         minus_half = const.tile([P, 1], F32)
         nc.vector.memset(minus_half[:], -0.5)
         eps_share = const.tile([P, 1], F32)

@@ -62,7 +62,11 @@ def tile_lstmcell2_w_kernel(
         w_planes = const.tile([P, GATES * H], U8, align_bytes=64)
         ident = const.tile([P, P], F32)
         make_identity(nc, ident[:])
-        for first, width, queue, words in ((0, H, nc.sync, I32), (H, 3 * H, nc.gpsimd, F32)):
+        for first, width, queue, words in (
+            (GATE_I * H, H, nc.sync, I32),
+            (GATE_F * H, 2 * H, nc.gpsimd, F32),
+            (GATE_G * H, H, nc.sync, I32),
+        ):
             nc.vector.memset(w_planes[:, first : first + width].bitcast(I32), 0)
             for quadrant in range(4):
                 queue.dma_start(

@@ -97,7 +97,6 @@ def tile_lstmcell2_w_kernel(
 
         for g in range(PASSES):
             load_pass(GATE_ORDER[0], g)
-        nc.sync.dma_start(out=c_sb[:], in_=c)
         def load_two_tiles(gate, first_tile):
             chunk = weights.tile([P, 2, 2 * N_TILE], U32, align_bytes=64)
             first = gate * H + first_tile * N_TILE
@@ -110,6 +109,8 @@ def tile_lstmcell2_w_kernel(
                     w_words[(gate, g, first_tile + t)] = chunk[:, g - 2, t * N_TILE : (t + 1) * N_TILE]
 
         for gate in GATE_ORDER[1:]:
+            if gate == GATE_ORDER[-1]:
+                nc.sync.dma_start(out=c_sb[:], in_=c)
             for g in range(2):
                 load_pass(gate, g)
             load_two_tiles(gate, 0)
@@ -133,6 +134,8 @@ def tile_lstmcell2_w_kernel(
 
         minus_half = const.tile([P, 1], F32)
         nc.vector.memset(minus_half[:], -0.5)
+        ident_bf = const.tile([P, P], BF16)
+        nc.gpsimd.tensor_copy(out=ident_bf[:], in_=ident[:])
         eps_share = const.tile([P, 1], F32)
         nc.vector.memset(eps_share[:], EPS / (TILES - 1))
 
@@ -188,24 +191,6 @@ def tile_lstmcell2_w_kernel(
                 copy_out = nc.vector.tensor_copy if half == 0 else nc.scalar.copy
                 copy_out(out=bias_all[:, first : first + BANK_CHANNELS].bitcast(F32), in_=bank[:])
 
-        def gate_matmul(gate, steps, before_gain):
-            acc = [acc_psum.tile([P, N_TILE], F32, name="acc") for t in range(TILES)]
-            gain = None
-            for index, (g, t) in enumerate(steps):
-                if index == len(steps) - before_gain:
-                    gain = spread_gate(GAIN_ROWS, gate)
-                nc.tensor.matmul_mx(
-                    out=acc[t][:],
-                    lhsT=h_codes[:, g * P : (g + 1) * P].bitcast(FP8X4),
-                    lhsT_scale=h_scales[:, g * P : (g + 1) * P],
-                    rhs=w_words[(gate, g, t)].bitcast(FP8X4),
-                    rhs_scale=w_planes[4 * g : P, gate * H + t * N_TILE : gate * H + (t + 1) * N_TILE],
-                    start=(g == 0),
-                    stop=(g == PASSES - 1),
-                )
-            shift = spread_gate(SHIFT_ROWS, gate)
-            return acc, gain, shift
-
         by_pass = [(g, t) for g in range(PASSES) for t in range(TILES)]
         two_tiles_at_the_end = [(g, t) for g in (0, 1) for t in range(TILES)] + [
             (g, t) for t in range(TILES) for g in (2, 3)
@@ -216,87 +201,146 @@ def tile_lstmcell2_w_kernel(
             + [(2, 2), (2, 3), (3, 2), (3, 3)]
         )
 
-        def gate_centred(gate, acc, gain, centred):
-            lin = work.tile([P, H], F32)
-            squares = work.tile([P, N_TILE], BF16)
-            tile_sums = stats.tile([P, TILES], F32)
-            tile_sq_sums = stats.tile([P, TILES], F32)
-            neg_centre = stats.tile([P, 1], F32)
-            early_sum = stats.tile([P, 1], F32)
-            early_sq = stats.tile([P, 1], F32)
-            copied = stats.tile([P, TILES - 1], F32)
-            for t in range(TILES):
-                cols = slice(t * N_TILE, (t + 1) * N_TILE)
-                nc.vector.scalar_tensor_tensor(
-                    out=lin[:, cols],
-                    in0=acc[t][:],
-                    scalar=1.0,
-                    in1=bias_all[:, gate * H + t * N_TILE : gate * H + (t + 1) * N_TILE],
-                    op0=ALU.mult,
-                    op1=ALU.add,
-                    accum_out=tile_sums[:, t : t + 1],
+        def passes(gate, acc, steps):
+            for g, t in steps:
+                nc.tensor.matmul_mx(
+                    out=acc[t][:],
+                    lhsT=h_codes[:, g * P : (g + 1) * P].bitcast(FP8X4),
+                    lhsT_scale=h_scales[:, g * P : (g + 1) * P],
+                    rhs=w_words[(gate, g, t)].bitcast(FP8X4),
+                    rhs_scale=w_planes[4 * g : P, gate * H + t * N_TILE : gate * H + (t + 1) * N_TILE],
+                    start=(g == 0),
+                    stop=(g == PASSES - 1),
                 )
-                if t == 0:
-                    nc.scalar.mul(out=neg_centre[:], in_=tile_sums[:, 0:1], mul=-1.0 / N_TILE)
-                nc.scalar.activation(
-                    out=squares[:], in_=lin[:, cols], func=ACT.Square, bias=neg_centre[:], scale=1.0,
-                    accum_out=tile_sq_sums[:, t : t + 1],
-                )
-                if t == TILES - 2:
-                    nc.vector.tensor_reduce(out=early_sum[:], in_=tile_sums[:, 0 : TILES - 1], axis=AX.X, op=ALU.add)
-                    nc.scalar.activation(
-                        out=copied[:], in_=tile_sq_sums[:, 0 : TILES - 1], func=ACT.Identity,
-                        bias=eps_share[:], scale=1.0 / H, accum_out=early_sq[:],
-                    )
-            neg_mean = stats.tile([P, 1], F32)
-            nc.vector.tensor_scalar(
-                out=neg_mean[:], in0=tile_sums[:, TILES - 1 : TILES], scalar1=early_sum[:], scalar2=-1.0 / H,
-                op0=ALU.add, op1=ALU.mult,
-            )
-            for half in range(BANKS_PER_GATE):
-                cols = slice(half * BANK_CHANNELS, (half + 1) * BANK_CHANNELS)
-                nc.vector.scalar_tensor_tensor(
-                    out=centred[:, cols],
-                    in0=lin[:, cols],
-                    scalar=neg_mean[:],
-                    in1=gain[half][:].bitcast(BF16),
-                    op0=ALU.add,
-                    op1=ALU.mult,
-                )
-            offset_sq = stats.tile([P, 1], F32)
-            nc.scalar.activation(
-                out=offset_sq[:], in_=neg_mean[:], func=ACT.Square, bias=neg_centre[:], scale=-1.0
-            )
-            early_less = stats.tile([P, 1], F32)
-            nc.scalar.activation(
-                out=early_less[:], in_=offset_sq[:], func=ACT.Identity, bias=early_sq[:], scale=-1.0
-            )
-            var_eps = stats.tile([P, 1], F32)
-            nc.scalar.activation(
-                out=var_eps[:], in_=tile_sq_sums[:, TILES - 1 : TILES], func=ACT.Identity, bias=early_less[:],
-                scale=1.0 / H,
-            )
-            return var_eps
 
-        def inverse_root(var_eps):
-            rstd = stats.tile([P, 1], F32)
-            nc.gpsimd.tensor_tensor(out=rstd[:], in0=var_eps[:], in1=minus_half[:], op=ALU.pow)
-            return rstd
+        def new_acc():
+            return [acc_psum.tile([P, N_TILE], F32, name="acc") for t in range(TILES)]
 
-        def scale_and_shift(centred, rstd, shift, first, width):
-            cols = slice(first, first + width)
-            in_bank = first % BANK_CHANNELS
+        def tile_cols(t):
+            return slice(t * N_TILE, (t + 1) * N_TILE)
+
+        def new_stats(gate, acc):
+            return {
+                "gate": gate,
+                "acc": acc,
+                "lin": work.tile([P, H], F32, name="lin"),
+                "squares": work.tile([P, N_TILE], BF16, name="squares"),
+                "sums": stats.tile([P, TILES], F32, name="sums"),
+                "sq_sums": stats.tile([P, TILES], F32, name="sq_sums"),
+                "neg_centre": stats.tile([P, 1], F32, name="neg_centre"),
+                "early_sum": stats.tile([P, 1], F32, name="early_sum"),
+                "early_sq": stats.tile([P, 1], F32, name="early_sq"),
+                "copied": stats.tile([P, TILES - 1], F32, name="copied"),
+                "neg_mean": stats.tile([P, 1], F32, name="neg_mean"),
+                "offset_sq": stats.tile([P, 1], F32, name="offset_sq"),
+                "early_less": stats.tile([P, 1], F32, name="early_less"),
+                "var_eps": stats.tile([P, 1], F32, name="var_eps"),
+                "rstd": stats.tile([P, 1], F32, name="rstd"),
+            }
+
+        def add_bias(st, t):
+            gate = st["gate"]
             nc.vector.scalar_tensor_tensor(
-                out=centred[:, cols],
-                in0=centred[:, cols],
-                scalar=rstd[:],
-                in1=shift[first // BANK_CHANNELS][:].bitcast(BF16)[:, in_bank : in_bank + width],
+                out=st["lin"][:, tile_cols(t)],
+                in0=st["acc"][t][:],
+                scalar=1.0,
+                in1=bias_all[:, gate * H + t * N_TILE : gate * H + (t + 1) * N_TILE],
+                op0=ALU.mult,
+                op1=ALU.add,
+                accum_out=st["sums"][:, t : t + 1],
+            )
+            if t == TILES - 2:
+                nc.vector.tensor_reduce(
+                    out=st["early_sum"][:], in_=st["sums"][:, 0 : TILES - 1], axis=AX.X, op=ALU.add
+                )
+
+        def square(st, t):
+            if t == 0:
+                nc.scalar.mul(out=st["neg_centre"][:], in_=st["sums"][:, 0:1], mul=-1.0 / N_TILE)
+            nc.scalar.activation(
+                out=st["squares"][:], in_=st["lin"][:, tile_cols(t)], func=ACT.Square, bias=st["neg_centre"][:],
+                scale=1.0, accum_out=st["sq_sums"][:, t : t + 1],
+            )
+            if t == TILES - 2:
+                nc.scalar.activation(
+                    out=st["copied"][:], in_=st["sq_sums"][:, 0 : TILES - 1], func=ACT.Identity,
+                    bias=eps_share[:], scale=1.0 / H, accum_out=st["early_sq"][:],
+                )
+
+        def mean(st):
+            nc.vector.tensor_scalar(
+                out=st["neg_mean"][:], in0=st["sums"][:, TILES - 1 : TILES], scalar1=st["early_sum"][:],
+                scalar2=-1.0 / H, op0=ALU.add, op1=ALU.mult,
+            )
+
+        def variance(st):
+            nc.scalar.activation(
+                out=st["offset_sq"][:], in_=st["neg_mean"][:], func=ACT.Square, bias=st["neg_centre"][:], scale=-1.0
+            )
+            nc.scalar.activation(
+                out=st["early_less"][:], in_=st["offset_sq"][:], func=ACT.Identity, bias=st["early_sq"][:], scale=-1.0
+            )
+            nc.scalar.activation(
+                out=st["var_eps"][:], in_=st["sq_sums"][:, TILES - 1 : TILES], func=ACT.Identity,
+                bias=st["early_less"][:], scale=1.0 / H,
+            )
+
+        def inverse_root(st):
+            nc.gpsimd.tensor_tensor(out=st["rstd"][:], in0=st["var_eps"][:], in1=minus_half[:], op=ALU.pow)
+
+        def centre(st, gain, tile, first, width):
+            half, in_bank = divmod(first, BANK_CHANNELS)
+            nc.vector.scalar_tensor_tensor(
+                out=tile[:, first : first + width],
+                in0=st["lin"][:, first : first + width],
+                scalar=st["neg_mean"][:],
+                in1=gain[half][:].bitcast(BF16)[:, in_bank : in_bank + width],
+                op0=ALU.add,
+                op1=ALU.mult,
+            )
+
+        def scale_and_shift(st, shift, tile, first, width):
+            half, in_bank = divmod(first, BANK_CHANNELS)
+            nc.vector.scalar_tensor_tensor(
+                out=tile[:, first : first + width],
+                in0=tile[:, first : first + width],
+                scalar=st["rstd"][:],
+                in1=shift[half][:].bitcast(BF16)[:, in_bank : in_bank + width],
                 op0=ALU.mult,
                 op1=ALU.add,
             )
 
+        def diagonal_of(st):
+            diagonal = stats.tile([P, P], F32)
+            nc.gpsimd.tensor_scalar(
+                out=diagonal[:], in0=ident[:], scalar1=st["rstd"][:], scalar2=0.0, op0=ALU.mult, op1=ALU.add
+            )
+            return diagonal
+
+        def normalise(gate, tile, diagonal, t, bank):
+            for half in range(N_TILE // ROW):
+                cols = slice(half * ROW, (half + 1) * ROW)
+                row = SHIFT_ROWS + gate * ROWS_PER_GATE + t * (N_TILE // ROW) + half
+                nc.tensor.matmul(
+                    out=bank[:, cols],
+                    lhsT=ident_bf[:, row : row + 1].to_broadcast([P, P]),
+                    rhs=vec_rows[:],
+                    start=True,
+                    stop=False,
+                )
+                first = t * N_TILE + half * ROW
+                nc.tensor.matmul(
+                    out=bank[:, cols], lhsT=diagonal[:], rhs=tile[:, first : first + ROW], start=False, stop=True
+                )
+
         def squash(tile, func, first, width):
             nc.scalar.activation(out=tile[:, first : first + width], in_=tile[:, first : first + width], func=func)
+
+        def squash_bank(tile, bank, func, t):
+            nc.scalar.activation(out=tile[:, tile_cols(t)], in_=bank[:], func=func)
+
+        def product(engine, out, in0, in1, t, op=ALU.mult):
+            engine.tensor_tensor(out=out[:, tile_cols(t)], in0=in0[:, tile_cols(t)], in1=in1[:, tile_cols(t)], op=op)
 
         gate_i = const.tile([P, H], F32)
         gate_g = const.tile([P, H], F32)
@@ -305,74 +349,98 @@ def tile_lstmcell2_w_kernel(
         c_new = const.tile([P, H], F32)
         tanh_c = const.tile([P, H], F32)
 
-        acc, gain, shift = gate_matmul(GATE_I, by_pass, TILES)
-        rstd = inverse_root(gate_centred(GATE_I, acc, gain, gate_i))
-        for first in range(0, H, BANK_CHANNELS):
-            scale_and_shift(gate_i, rstd, shift, first, BANK_CHANNELS)
-            squash(gate_i, ACT.Sigmoid, first, BANK_CHANNELS)
+        def whole_gate(gate, tile, func, steps, gain_before):
+            acc = new_acc()
+            passes(gate, acc, steps[:-gain_before])
+            gain = spread_gate(GAIN_ROWS, gate)
+            passes(gate, acc, steps[-gain_before:])
+            shift = spread_gate(SHIFT_ROWS, gate)
+            st = new_stats(gate, acc)
+            for t in range(TILES):
+                add_bias(st, t)
+                square(st, t)
+            mean(st)
+            variance(st)
+            inverse_root(st)
+            for first in range(0, H, BANK_CHANNELS):
+                centre(st, gain, tile, first, BANK_CHANNELS)
+            for first in range(0, H, BANK_CHANNELS):
+                scale_and_shift(st, shift, tile, first, BANK_CHANNELS)
+                squash(tile, func, first, BANK_CHANNELS)
 
-        acc, gain, shift = gate_matmul(GATE_G, two_tiles_at_the_end, TILES)
-        rstd = inverse_root(gate_centred(GATE_G, acc, gain, gate_g))
+        whole_gate(GATE_I, gate_i, ACT.Sigmoid, by_pass, TILES)
+        whole_gate(GATE_G, gate_g, ACT.Tanh, two_tiles_at_the_end, TILES)
         for first in range(0, H, BANK_CHANNELS):
             cols = slice(first, first + BANK_CHANNELS)
-            scale_and_shift(gate_g, rstd, shift, first, BANK_CHANNELS)
-            squash(gate_g, ACT.Tanh, first, BANK_CHANNELS)
             nc.gpsimd.tensor_tensor(out=gate_i[:, cols], in0=gate_i[:, cols], in1=gate_g[:, cols], op=ALU.mult)
 
-        acc, gain, shift = gate_matmul(GATE_F, two_tiles_at_the_end, TILES)
-        rstd = inverse_root(gate_centred(GATE_F, acc, gain, gate_f))
-        for first, width in SMALL_FIRST:
-            cols = slice(first, first + width)
-            scale_and_shift(gate_f, rstd, shift, first, width)
-            squash(gate_f, ACT.Sigmoid, first, width)
-            nc.gpsimd.tensor_tensor(out=gate_f[:, cols], in0=gate_f[:, cols], in1=c_sb[:, cols], op=ALU.mult)
-
-        def new_cell(first, width):
-            cols = slice(first, first + width)
-            nc.gpsimd.tensor_tensor(out=c_new[:, cols], in0=gate_f[:, cols], in1=gate_i[:, cols], op=ALU.add)
-
-        def tanh_cell(first, width):
-            cols = slice(first, first + width)
-            nc.scalar.activation(out=tanh_c[:, cols], in_=c_new[:, cols], func=ACT.Tanh)
-
-        def store_cell(tile_first):
-            cols = slice(tile_first, tile_first + N_TILE)
-            nc.scalar.dma_start(out=out_1[:, cols], in_=c_new[:, cols])
-
-        def sigmoid_o(piece):
-            squash(gate_o, ACT.Sigmoid, piece[0], piece[1])
-
-        def output(first, width):
-            cols = slice(first, first + width)
-            nc.vector.tensor_tensor(out=gate_o[:, cols], in0=gate_o[:, cols], in1=tanh_c[:, cols], op=ALU.mult)
-
-        acc, gain, shift = gate_matmul(GATE_O, tiles_at_the_end, 2 * TILES)
-        var_eps = gate_centred(GATE_O, acc, gain, gate_o)
-        halves = ((3 * N_TILE, N_TILE // 2), (3 * N_TILE + N_TILE // 2, N_TILE // 2))
-        new_cell(0, N_TILE)
-        rstd = inverse_root(var_eps)
-        new_cell(N_TILE, N_TILE)
-        new_cell(2 * N_TILE, N_TILE)
-        for first, width in halves:
-            new_cell(first, width)
-        for first, width in EQUAL:
-            scale_and_shift(gate_o, rstd, shift, first, width)
-        tanh_cell(0, N_TILE)
-        store_cell(0)
-        sigmoid_o(EQUAL[0])
-        tanh_cell(N_TILE, N_TILE)
-        store_cell(N_TILE)
-        sigmoid_o(EQUAL[1])
-        sigmoid_o(EQUAL[2])
-        tanh_cell(2 * N_TILE, N_TILE)
-        store_cell(2 * N_TILE)
-        sigmoid_o(EQUAL[3])
-        for first, width in halves:
-            tanh_cell(first, width)
-        store_cell(3 * N_TILE)
-        for first, width in EQUAL[:3]:
-            output(first, width)
-            nc.sync.dma_start(out=out_0[:, first : first + width], in_=gate_o[:, first : first + width])
-        for first, width in halves:
-            output(first, width)
-        nc.sync.dma_start(out=out_0[:, 3 * N_TILE : H], in_=gate_o[:, 3 * N_TILE : H])
+        acc = new_acc()
+        passes(GATE_F, acc, two_tiles_at_the_end[:-TILES])
+        gain = spread_gate(GAIN_ROWS, GATE_F)
+        passes(GATE_F, acc, two_tiles_at_the_end[-TILES:])
+        shift = spread_gate(SHIFT_ROWS, GATE_F)
+        st = new_stats(GATE_F, acc)
+        for t in range(TILES):
+            add_bias(st, t)
+            square(st, t)
+        mean(st)
+        variance(st)
+        inverse_root(st)
+        for first in range(0, H, BANK_CHANNELS):
+            centre(st, gain, gate_f, first, BANK_CHANNELS)
+        for t in range(TILES):
+            scale_and_shift(st, shift, gate_f, t * N_TILE, N_TILE)
+            squash(gate_f, ACT.Sigmoid, t * N_TILE, N_TILE)
+        acc = new_acc()
+        passes(GATE_O, acc, tiles_at_the_end[:TILES])
+        c_banks = []
+        for half in range(BANKS_PER_GATE):
+            bank = spread_psum.tile([P, BANK_CHANNELS], BF16, tag="bank")
+            for k in range(BANK_CHANNELS // N_TILE):
+                if 2 * half + k == 0:
+                    continue
+                nc.tensor.matmul(
+                    out=bank[:, k * N_TILE : (k + 1) * N_TILE], lhsT=ident_bf[:],
+                    rhs=c_sb[:, (2 * half + k) * N_TILE : (2 * half + k + 1) * N_TILE], start=True, stop=True,
+                )
+            c_banks.append(bank)
+        passes(GATE_O, acc, tiles_at_the_end[TILES : 2 * TILES])
+        passes(GATE_O, acc, tiles_at_the_end[2 * TILES :])
+        gain = spread_gate(GAIN_ROWS, GATE_O)
+        shift = spread_gate(SHIFT_ROWS, GATE_O)
+        product(nc.gpsimd, gate_f, gate_f, c_sb, 0)
+        for t in range(1, TILES):
+            nc.vector.tensor_tensor(
+                out=gate_f[:, tile_cols(t)], in0=gate_f[:, tile_cols(t)],
+                in1=c_banks[t // 2][:, (t % 2) * N_TILE : (t % 2 + 1) * N_TILE], op=ALU.mult,
+            )
+        st = new_stats(GATE_O, acc)
+        def tanh_cell(t):
+            nc.scalar.activation(out=tanh_c[:, tile_cols(t)], in_=c_new[:, tile_cols(t)], func=ACT.Tanh)
+            nc.scalar.dma_start(out=out_1[:, tile_cols(t)], in_=c_new[:, tile_cols(t)])
+        def add(engine, t):
+            product(engine, c_new, gate_f, gate_i, t, ALU.add)
+        def op3(t):
+            scale_and_shift(st, shift, gate_o, t * N_TILE, N_TILE)
+        def sig(t):
+            squash(gate_o, ACT.Sigmoid, t * N_TILE, N_TILE)
+        def out(engine, t):
+            product(engine, gate_o, gate_o, tanh_c, t)
+            nc.sync.dma_start(out=out_0[:, tile_cols(t)], in_=gate_o[:, tile_cols(t)])
+        for t in range(TILES): add(nc.gpsimd, t)
+        tanh_cell(0)
+        add_bias(st, 0); square(st, 0)
+        add_bias(st, 1); square(st, 1)
+        add_bias(st, 2); square(st, 2)
+        add_bias(st, 3); square(st, 3)
+        mean(st); variance(st)
+        inverse_root(st)
+        diagonal = diagonal_of(st)
+        for t in range(TILES): centre(st, gain, gate_o, t * N_TILE, N_TILE)
+        tanh_cell(1); tanh_cell(2); tanh_cell(3)
+        bank = acc_psum.tile([P, N_TILE], F32, name="acc")
+        normalise(GATE_O, gate_o, diagonal, 0, bank)
+        for t in (1, 2, 3): op3(t)
+        for t in (1, 2, 3): sig(t)
+        squash_bank(gate_o, bank, ACT.Sigmoid, 0)
+        for t in (1, 2, 3, 0): out(nc.vector, t)

@@ -63,9 +63,9 @@ def tile_lstmcell2_w_kernel(
         ident = const.tile([P, P], F32)
         make_identity(nc, ident[:])
         for first, width, queue, words in (
-            (GATE_I * H, H, nc.sync, I32),
+            (GATE_I * H, H, nc.gpsimd, F32),
+            (GATE_G * H, H, nc.gpsimd, F32),
             (GATE_F * H, 2 * H, nc.gpsimd, F32),
-            (GATE_G * H, H, nc.sync, I32),
         ):
             nc.vector.memset(w_planes[:, first : first + width].bitcast(I32), 0)
             for quadrant in range(4):
@@ -117,20 +117,19 @@ def tile_lstmcell2_w_kernel(
             if gate != GATE_ORDER[-1]:
                 load_two_tiles(gate, 2)
                 continue
-            half_pass = ends.tile([P, 2 * N_TILE], U32, align_bytes=64)
+            first = gate * H + 2 * N_TILE
+            tile_2 = ends.tile([P, 2, N_TILE], U32, align_bytes=64)
             nc.sync.dma_start(
-                out=half_pass[:].bitcast(I32),
-                in_=words_i32[2, :, gate * H + 2 * N_TILE : (gate + 1) * H],
+                out=tile_2[:].bitcast(I32),
+                in_=words_i32[2:4, :, first : first + N_TILE].rearrange("g p n -> p g n"),
             )
-            for t in (2, 3):
-                w_words[(gate, 2, t)] = half_pass[:, (t - 2) * N_TILE : (t - 1) * N_TILE]
-            for t in (2, 3):
-                piece = ends.tile([P, N_TILE], U32, align_bytes=64, name="piece%d" % t)
+            for g in (2, 3):
+                w_words[(gate, g, 2)] = tile_2[:, g - 2, :]
+                piece = ends.tile([P, N_TILE], U32, align_bytes=64, name="piece%d" % g)
                 nc.sync.dma_start(
-                    out=piece[:].bitcast(I32),
-                    in_=words_i32[3, :, gate * H + t * N_TILE : gate * H + (t + 1) * N_TILE],
+                    out=piece[:].bitcast(I32), in_=words_i32[g, :, first + N_TILE : first + 2 * N_TILE]
                 )
-                w_words[(gate, 3, t)] = piece[:]
+                w_words[(gate, g, 3)] = piece[:]
 
         minus_half = const.tile([P, 1], F32)
         nc.vector.memset(minus_half[:], -0.5)
@@ -151,6 +150,19 @@ def tile_lstmcell2_w_kernel(
                     bank[:, i * P : (i + 1) * P],
                     vec_cols[:, first_row + i : first_row + i + 1].to_broadcast([P, P]),
                     ident[:],
+                )
+            return bank
+
+        def pick_rows(vector_rows, gate, half):
+            bank = spread_psum.tile([P, BANK_CHANNELS], BF16, tag="bank")
+            for i in range(ROWS_PER_BANK):
+                row = vector_rows + gate * ROWS_PER_GATE + half * ROWS_PER_BANK + i
+                nc.tensor.matmul(
+                    out=bank[:, i * ROW : (i + 1) * ROW],
+                    lhsT=ident_bf[:, row : row + 1].to_broadcast([P, P]),
+                    rhs=vec_rows[:],
+                    start=True,
+                    stop=True,
                 )
             return bank
 
@@ -198,7 +210,7 @@ def tile_lstmcell2_w_kernel(
         tiles_at_the_end = (
             [(g, t) for g in (0, 1) for t in range(TILES)]
             + [(g, t) for t in (0, 1) for g in (2, 3)]
-            + [(2, 2), (2, 3), (3, 2), (3, 3)]
+            + [(g, t) for t in (2, 3) for g in (2, 3)]
         )
 
         def passes(gate, acc, steps):
@@ -224,7 +236,7 @@ def tile_lstmcell2_w_kernel(
                 "gate": gate,
                 "acc": acc,
                 "lin": work.tile([P, H], F32, name="lin"),
-                "squares": work.tile([P, N_TILE], BF16, name="squares"),
+                "squares": work.tile([P, 2, N_TILE], BF16, name="squares"),
                 "sums": stats.tile([P, TILES], F32, name="sums"),
                 "sq_sums": stats.tile([P, TILES], F32, name="sq_sums"),
                 "neg_centre": stats.tile([P, 1], F32, name="neg_centre"),
@@ -258,7 +270,7 @@ def tile_lstmcell2_w_kernel(
             if t == 0:
                 nc.scalar.mul(out=st["neg_centre"][:], in_=st["sums"][:, 0:1], mul=-1.0 / N_TILE)
             nc.scalar.activation(
-                out=st["squares"][:], in_=st["lin"][:, tile_cols(t)], func=ACT.Square, bias=st["neg_centre"][:],
+                out=st["squares"][:, t % 2, :], in_=st["lin"][:, tile_cols(t)], func=ACT.Square, bias=st["neg_centre"][:],
                 scale=1.0, accum_out=st["sq_sums"][:, t : t + 1],
             )
             if t == TILES - 2:
@@ -312,25 +324,25 @@ def tile_lstmcell2_w_kernel(
 
         def diagonal_of(st):
             diagonal = stats.tile([P, P], F32)
-            nc.gpsimd.tensor_scalar(
-                out=diagonal[:], in0=ident[:], scalar1=st["rstd"][:], scalar2=0.0, op0=ALU.mult, op1=ALU.add
-            )
+            nc.scalar.activation(out=diagonal[:], in_=ident[:], func=ACT.Copy, scale=st["rstd"][:])
             return diagonal
 
-        def normalise(gate, tile, diagonal, t, bank):
-            for half in range(N_TILE // ROW):
-                cols = slice(half * ROW, (half + 1) * ROW)
+        def open_with_shift(gate, t, banks):
+            for half, bank in enumerate(banks):
                 row = SHIFT_ROWS + gate * ROWS_PER_GATE + t * (N_TILE // ROW) + half
                 nc.tensor.matmul(
-                    out=bank[:, cols],
+                    out=bank[:, 0:ROW],
                     lhsT=ident_bf[:, row : row + 1].to_broadcast([P, P]),
                     rhs=vec_rows[:],
                     start=True,
                     stop=False,
                 )
+
+        def add_scaled(tile, diagonal, t, banks):
+            for half, bank in enumerate(banks):
                 first = t * N_TILE + half * ROW
                 nc.tensor.matmul(
-                    out=bank[:, cols], lhsT=diagonal[:], rhs=tile[:, first : first + ROW], start=False, stop=True
+                    out=bank[:, 0:ROW], lhsT=diagonal[:], rhs=tile[:, first : first + ROW], start=False, stop=True
                 )
 
         def squash(tile, func, first, width):
@@ -388,46 +400,65 @@ def tile_lstmcell2_w_kernel(
         inverse_root(st)
         for first in range(0, H, BANK_CHANNELS):
             centre(st, gain, gate_f, first, BANK_CHANNELS)
-        for t in range(TILES):
-            scale_and_shift(st, shift, gate_f, t * N_TILE, N_TILE)
-            squash(gate_f, ACT.Sigmoid, t * N_TILE, N_TILE)
+        st_f, shift_f = st, shift
         acc = new_acc()
         passes(GATE_O, acc, tiles_at_the_end[:TILES])
         c_banks = []
         for half in range(BANKS_PER_GATE):
             bank = spread_psum.tile([P, BANK_CHANNELS], BF16, tag="bank")
             for k in range(BANK_CHANNELS // N_TILE):
-                if 2 * half + k == 0:
-                    continue
                 nc.tensor.matmul(
                     out=bank[:, k * N_TILE : (k + 1) * N_TILE], lhsT=ident_bf[:],
                     rhs=c_sb[:, (2 * half + k) * N_TILE : (2 * half + k + 1) * N_TILE], start=True, stop=True,
                 )
             c_banks.append(bank)
         passes(GATE_O, acc, tiles_at_the_end[TILES : 2 * TILES])
+        gain = [pick_rows(GAIN_ROWS, GATE_O, 0)]
         passes(GATE_O, acc, tiles_at_the_end[2 * TILES :])
-        gain = spread_gate(GAIN_ROWS, GATE_O)
-        shift = spread_gate(SHIFT_ROWS, GATE_O)
-        product(nc.gpsimd, gate_f, gate_f, c_sb, 0)
-        for t in range(1, TILES):
+        gain.append(pick_rows(GAIN_ROWS, GATE_O, 1))
+        shift = [pick_rows(SHIFT_ROWS, GATE_O, 0)]
+        last_banks = [
+            spread_psum.tile([P, N_TILE], F32, tag="bank", name="last_bank"),
+            acc_psum.tile([P, N_TILE], F32, name="acc"),
+        ]
+        open_with_shift(GATE_O, 3, last_banks)
+        shift.append(pick_rows(SHIFT_ROWS, GATE_O, 1))
+        def f_times_c(t):
             nc.vector.tensor_tensor(
                 out=gate_f[:, tile_cols(t)], in0=gate_f[:, tile_cols(t)],
                 in1=c_banks[t // 2][:, (t % 2) * N_TILE : (t % 2 + 1) * N_TILE], op=ALU.mult,
             )
+        shift_late = work.tile([P, N_TILE], BF16)
+        nc.scalar.copy(
+            out=shift_late[:].bitcast(F32), in_=shift_f[1][:, N_TILE // 2 : N_TILE]
+        )
+        late = tile_cols(3)
+        nc.scalar.activation(out=gate_f[:, late], in_=gate_f[:, late], func=ACT.Copy, scale=st_f["rstd"][:])
+        nc.gpsimd.tensor_tensor(out=gate_f[:, late], in0=gate_f[:, late], in1=shift_late[:], op=ALU.add)
+        for t in range(3):
+            scale_and_shift(st_f, shift_f, gate_f, t * N_TILE, N_TILE)
+            squash(gate_f, ACT.Sigmoid, t * N_TILE, N_TILE)
+        squash(gate_f, ACT.Sigmoid, 3 * N_TILE, N_TILE)
+        f_times_c(0)
+        f_times_c(1)
+        f_times_c(2)
+        f_times_c(3)
         st = new_stats(GATE_O, acc)
         def tanh_cell(t):
             nc.scalar.activation(out=tanh_c[:, tile_cols(t)], in_=c_new[:, tile_cols(t)], func=ACT.Tanh)
-            nc.scalar.dma_start(out=out_1[:, tile_cols(t)], in_=c_new[:, tile_cols(t)])
+            nc.sync.dma_start(out=out_1[:, tile_cols(t)], in_=c_new[:, tile_cols(t)])
         def add(engine, t):
             product(engine, c_new, gate_f, gate_i, t, ALU.add)
         def op3(t):
             scale_and_shift(st, shift, gate_o, t * N_TILE, N_TILE)
         def sig(t):
             squash(gate_o, ACT.Sigmoid, t * N_TILE, N_TILE)
-        def out(engine, t):
-            product(engine, gate_o, gate_o, tanh_c, t)
-            nc.sync.dma_start(out=out_0[:, tile_cols(t)], in_=gate_o[:, tile_cols(t)])
-        for t in range(TILES): add(nc.gpsimd, t)
+        def out(first, width):
+            cols = slice(first, first + width)
+            nc.vector.tensor_tensor(out=gate_o[:, cols], in0=gate_o[:, cols], in1=tanh_c[:, cols], op=ALU.mult)
+            nc.sync.dma_start(out=out_0[:, cols], in_=gate_o[:, cols])
+        for t in range(TILES):
+            add(nc.gpsimd, t)
         tanh_cell(0)
         add_bias(st, 0); square(st, 0)
         add_bias(st, 1); square(st, 1)
@@ -435,12 +466,16 @@ def tile_lstmcell2_w_kernel(
         add_bias(st, 3); square(st, 3)
         mean(st); variance(st)
         inverse_root(st)
+        for t in (0, 1, 3, 2): centre(st, gain, gate_o, t * N_TILE, N_TILE)
+        tanh_cell(1)
+        tanh_cell(2)
         diagonal = diagonal_of(st)
-        for t in range(TILES): centre(st, gain, gate_o, t * N_TILE, N_TILE)
-        tanh_cell(1); tanh_cell(2); tanh_cell(3)
-        bank = acc_psum.tile([P, N_TILE], F32, name="acc")
-        normalise(GATE_O, gate_o, diagonal, 0, bank)
-        for t in (1, 2, 3): op3(t)
-        for t in (1, 2, 3): sig(t)
-        squash_bank(gate_o, bank, ACT.Sigmoid, 0)
-        for t in (1, 2, 3, 0): out(nc.vector, t)
+        tanh_cell(3)
+        add_scaled(gate_o, diagonal, 3, last_banks)
+        for t in (0, 1, 2): op3(t)
+        for t in (0, 1, 2): sig(t)
+        for half, bank in enumerate(last_banks):
+            first = 3 * N_TILE + half * ROW
+            nc.scalar.activation(out=gate_o[:, first : first + ROW], in_=bank[:, 0:ROW], func=ACT.Sigmoid)
+        for t in range(TILES - 1): out(t * N_TILE, N_TILE)
+        for half in range(2): out(3 * N_TILE + half * ROW, ROW)

from contextlib import ExitStack

import concourse.mybir as mybir
from concourse.masks import make_identity

F32 = mybir.dt.float32
BF16 = mybir.dt.bfloat16
I32 = mybir.dt.int32
U32 = mybir.dt.uint32
U8 = mybir.dt.uint8
FP8X4 = mybir.dt.float8_e4m3fn_x4
ALU = mybir.AluOpType
ACT = mybir.ActivationFunctionType
AX = mybir.AxisListType

P = 128
H = 2048
GATES = 4
PACK = 4
K_PASS = P * PACK
PASSES = H // K_PASS
N_TILE = 512
TILES = H // N_TILE
EPS = 1e-5

ROW = 256
ROWS_PER_VECTOR = GATES * H // ROW
ROWS_PER_GATE = H // ROW
ROWS_PER_BANK = N_TILE // P
BANK_CHANNELS = ROWS_PER_BANK * ROW
BANKS_PER_GATE = H // BANK_CHANNELS
BIAS_ROWS, GAIN_ROWS, SHIFT_ROWS = 0, ROWS_PER_VECTOR, 2 * ROWS_PER_VECTOR

GATE_I, GATE_F, GATE_O, GATE_G = 0, 1, 2, 3
GATE_ORDER = (GATE_I, GATE_G, GATE_F, GATE_O)

WEIGHT_BUFS = 3 * PASSES

SMALL_FIRST = ((0, 256), (256, 256), (512, 512), (1024, 512), (1536, 512))
EQUAL = ((0, 512), (512, 512), (1024, 512), (1536, 512))

FLOPS = 2 * P * H * GATES * H


def tile_lstmcell2_w_kernel(
    tc, x, h, c, W_words, W_scales, b, gn_weight, gn_bias, out_0, out_1
):
    nc = tc.nc
    with ExitStack() as stack:
        stack.enter_context(tc.manual_schedule())
        const = stack.enter_context(tc.tile_pool(name="const", bufs=1))
        weights = stack.enter_context(tc.tile_pool(name="weights", bufs=WEIGHT_BUFS))
        ends = stack.enter_context(tc.tile_pool(name="ends", bufs=2))
        work = stack.enter_context(tc.tile_pool(name="work", bufs=2))
        stats = stack.enter_context(tc.tile_pool(name="stats", bufs=2))
        spread_psum = stack.enter_context(tc.psum_pool(name="spread_psum", bufs=4))
        acc_psum = stack.enter_context(tc.psum_pool(name="acc_psum", bufs=TILES))

        h_sb = const.tile([P, H], BF16)
        nc.sync.dma_start(out=h_sb[:], in_=h)

        w_planes = const.tile([P, GATES * H], U8, align_bytes=64)
        ident = const.tile([P, P], F32)
        make_identity(nc, ident[:])
        for first, width, queue, words in (
            (GATE_I * H, H, nc.gpsimd, F32),
            (GATE_G * H, H, nc.gpsimd, F32),
            (GATE_F * H, 2 * H, nc.gpsimd, F32),
        ):
            nc.vector.memset(w_planes[:, first : first + width].bitcast(I32), 0)
            for quadrant in range(4):
                queue.dma_start(
                    out=w_planes[32 * quadrant : 32 * quadrant + 16, first : first + width].bitcast(words),
                    in_=W_scales.bitcast(words)[:, 4 * quadrant : 4 * quadrant + 4, first // 4 : (first + width) // 4],
                )

        vec_rows = const.tile([P, ROW], BF16)
        nc.vector.memset(vec_rows[3 * ROWS_PER_VECTOR : P, :], 0.0)
        for first_row, vector in ((BIAS_ROWS, b), (GAIN_ROWS, gn_weight), (SHIFT_ROWS, gn_bias)):
            nc.sync.dma_start(
                out=vec_rows[first_row : first_row + ROWS_PER_VECTOR, :],
                in_=vector.rearrange("(r w) -> r w", w=ROW),
            )

        words_i32 = W_words.rearrange("g p n t -> g p (n t)").bitcast(I32)
        c_sb = const.tile([P, H], BF16)
        w_words = {}

        def load_pass(gate, g):
            chunk = weights.tile([P, TILES, N_TILE], U32, align_bytes=64)
            nc.sync.dma_start(
                out=chunk[:].rearrange("p t n -> p (t n)").bitcast(I32),
                in_=words_i32[g, :, gate * H : (gate + 1) * H],
            )
            for t in range(TILES):
                w_words[(gate, g, t)] = chunk[:, t, :]

        for g in range(PASSES):
            load_pass(GATE_ORDER[0], g)
        def load_two_tiles(gate, first_tile):
            chunk = weights.tile([P, 2, 2 * N_TILE], U32, align_bytes=64)
            first = gate * H + first_tile * N_TILE
            nc.sync.dma_start(
                out=chunk[:].bitcast(I32),
                in_=words_i32[2:4, :, first : first + 2 * N_TILE].rearrange("g p n -> p g n"),
            )
            for g in (2, 3):
                for t in (0, 1):
                    w_words[(gate, g, first_tile + t)] = chunk[:, g - 2, t * N_TILE : (t + 1) * N_TILE]

        for gate in GATE_ORDER[1:]:
            if gate == GATE_ORDER[-1]:
                nc.sync.dma_start(out=c_sb[:], in_=c)
            for g in range(2):
                load_pass(gate, g)
            load_two_tiles(gate, 0)
            if gate != GATE_ORDER[-1]:
                load_two_tiles(gate, 2)
                continue
            first = gate * H + 2 * N_TILE
            tile_2 = ends.tile([P, 2, N_TILE], U32, align_bytes=64)
            nc.sync.dma_start(
                out=tile_2[:].bitcast(I32),
                in_=words_i32[2:4, :, first : first + N_TILE].rearrange("g p n -> p g n"),
            )
            for g in (2, 3):
                w_words[(gate, g, 2)] = tile_2[:, g - 2, :]
                piece = ends.tile([P, N_TILE], U32, align_bytes=64, name="piece%d" % g)
                nc.sync.dma_start(
                    out=piece[:].bitcast(I32), in_=words_i32[g, :, first + N_TILE : first + 2 * N_TILE]
                )
                w_words[(gate, g, 3)] = piece[:]

        minus_half = const.tile([P, 1], F32)
        nc.vector.memset(minus_half[:], -0.5)
        ident_bf = const.tile([P, P], BF16)
        nc.gpsimd.tensor_copy(out=ident_bf[:], in_=ident[:])
        eps_share = const.tile([P, 1], F32)
        nc.vector.memset(eps_share[:], EPS / (TILES - 1))

        vec_cols_ps = spread_psum.tile([P, P], F32, tag="bank")
        nc.tensor.transpose(vec_cols_ps[:], vec_rows[:].bitcast(F32), ident[:])
        vec_cols = const.tile([P, P], F32)
        nc.vector.tensor_copy(out=vec_cols[:], in_=vec_cols_ps[:])

        def spread_rows(first_row):
            bank = spread_psum.tile([P, ROWS_PER_BANK * P], F32, tag="bank")
            for i in range(ROWS_PER_BANK):
                nc.tensor.transpose(
                    bank[:, i * P : (i + 1) * P],
                    vec_cols[:, first_row + i : first_row + i + 1].to_broadcast([P, P]),
                    ident[:],
                )
            return bank

        def pick_rows(vector_rows, gate, half):
            bank = spread_psum.tile([P, BANK_CHANNELS], BF16, tag="bank")
            for i in range(ROWS_PER_BANK):
                row = vector_rows + gate * ROWS_PER_GATE + half * ROWS_PER_BANK + i
                nc.tensor.matmul(
                    out=bank[:, i * ROW : (i + 1) * ROW],
                    lhsT=ident_bf[:, row : row + 1].to_broadcast([P, P]),
                    rhs=vec_rows[:],
                    start=True,
                    stop=True,
                )
            return bank

        def spread_gate(vector_rows, gate):
            return [
                spread_rows(vector_rows + gate * ROWS_PER_GATE + half * ROWS_PER_BANK)
                for half in range(BANKS_PER_GATE)
            ]

        h_words = h_sb[:].bitcast(F32)
        grouped = const.tile([P, PASSES, P, PACK], BF16, align_bytes=64)
        grouped_words = grouped[:].bitcast(F32)
        for pair in range(PASSES // 2):
            h_t = spread_psum.tile([P, 2, 2, P], F32, tag="bank")
            for g2 in range(2):
                g = 2 * pair + g2
                for u in range(2):
                    nc.tensor.transpose(
                        h_t[:, g2, u, :], h_words[:, 256 * g + u : 256 * (g + 1) : 2], ident[:]
                    )
            copy_out = nc.vector.tensor_copy if pair == 0 else nc.scalar.copy
            copy_out(
                out=grouped_words[:, 2 * pair : 2 * pair + 2, :, :],
                in_=h_t[:].rearrange("p g u m -> p g m u"),
            )
        h_codes = const.tile([P, PASSES * P], U32, align_bytes=64)
        h_scales = const.tile([P, PASSES * P], U8, align_bytes=64)
        nc.vector.quantize_mx(
            out=h_codes[:].bitcast(FP8X4),
            scales=h_scales[:],
            in_=grouped[:].rearrange("p g m t -> p (g m t)"),
        )

        bias_all = const.tile([P, GATES * H], BF16)
        for gate in GATE_ORDER:
            for half, bank in enumerate(spread_gate(BIAS_ROWS, gate)):
                first = gate * H + half * BANK_CHANNELS
                copy_out = nc.vector.tensor_copy if half == 0 else nc.scalar.copy
                copy_out(out=bias_all[:, first : first + BANK_CHANNELS].bitcast(F32), in_=bank[:])

        by_pass = [(g, t) for g in range(PASSES) for t in range(TILES)]
        two_tiles_at_the_end = [(g, t) for g in (0, 1) for t in range(TILES)] + [
            (g, t) for t in range(TILES) for g in (2, 3)
        ]
        tiles_at_the_end = (
            [(g, t) for g in (0, 1) for t in range(TILES)]
            + [(g, t) for t in (0, 1) for g in (2, 3)]
            + [(g, t) for t in (2, 3) for g in (2, 3)]
        )

        def passes(gate, acc, steps):
            for g, t in steps:
                nc.tensor.matmul_mx(
                    out=acc[t][:],
                    lhsT=h_codes[:, g * P : (g + 1) * P].bitcast(FP8X4),
                    lhsT_scale=h_scales[:, g * P : (g + 1) * P],
                    rhs=w_words[(gate, g, t)].bitcast(FP8X4),
                    rhs_scale=w_planes[4 * g : P, gate * H + t * N_TILE : gate * H + (t + 1) * N_TILE],
                    start=(g == 0),
                    stop=(g == PASSES - 1),
                )

        def new_acc():
            return [acc_psum.tile([P, N_TILE], F32, name="acc") for t in range(TILES)]

        def tile_cols(t):
            return slice(t * N_TILE, (t + 1) * N_TILE)

        def new_stats(gate, acc):
            return {
                "gate": gate,
                "acc": acc,
                "lin": work.tile([P, H], F32, name="lin"),
                "squares": work.tile([P, 2, N_TILE], BF16, name="squares"),
                "sums": stats.tile([P, TILES], F32, name="sums"),
                "sq_sums": stats.tile([P, TILES], F32, name="sq_sums"),
                "neg_centre": stats.tile([P, 1], F32, name="neg_centre"),
                "early_sum": stats.tile([P, 1], F32, name="early_sum"),
                "early_sq": stats.tile([P, 1], F32, name="early_sq"),
                "copied": stats.tile([P, TILES - 1], F32, name="copied"),
                "neg_mean": stats.tile([P, 1], F32, name="neg_mean"),
                "offset_sq": stats.tile([P, 1], F32, name="offset_sq"),
                "early_less": stats.tile([P, 1], F32, name="early_less"),
                "var_eps": stats.tile([P, 1], F32, name="var_eps"),
                "rstd": stats.tile([P, 1], F32, name="rstd"),
            }

        def add_bias(st, t):
            gate = st["gate"]
            nc.vector.scalar_tensor_tensor(
                out=st["lin"][:, tile_cols(t)],
                in0=st["acc"][t][:],
                scalar=1.0,
                in1=bias_all[:, gate * H + t * N_TILE : gate * H + (t + 1) * N_TILE],
                op0=ALU.mult,
                op1=ALU.add,
                accum_out=st["sums"][:, t : t + 1],
            )
            if t == TILES - 2:
                nc.vector.tensor_reduce(
                    out=st["early_sum"][:], in_=st["sums"][:, 0 : TILES - 1], axis=AX.X, op=ALU.add
                )

        def square(st, t):
            if t == 0:
                nc.scalar.mul(out=st["neg_centre"][:], in_=st["sums"][:, 0:1], mul=-1.0 / N_TILE)
            nc.scalar.activation(
                out=st["squares"][:, t % 2, :], in_=st["lin"][:, tile_cols(t)], func=ACT.Square, bias=st["neg_centre"][:],
                scale=1.0, accum_out=st["sq_sums"][:, t : t + 1],
            )
            if t == TILES - 2:
                nc.scalar.activation(
                    out=st["copied"][:], in_=st["sq_sums"][:, 0 : TILES - 1], func=ACT.Identity,
                    bias=eps_share[:], scale=1.0 / H, accum_out=st["early_sq"][:],
                )

        def mean(st):
            nc.vector.tensor_scalar(
                out=st["neg_mean"][:], in0=st["sums"][:, TILES - 1 : TILES], scalar1=st["early_sum"][:],
                scalar2=-1.0 / H, op0=ALU.add, op1=ALU.mult,
            )

        def variance(st):
            nc.scalar.activation(
                out=st["offset_sq"][:], in_=st["neg_mean"][:], func=ACT.Square, bias=st["neg_centre"][:], scale=-1.0
            )
            nc.scalar.activation(
                out=st["early_less"][:], in_=st["offset_sq"][:], func=ACT.Identity, bias=st["early_sq"][:], scale=-1.0
            )
            nc.scalar.activation(
                out=st["var_eps"][:], in_=st["sq_sums"][:, TILES - 1 : TILES], func=ACT.Identity,
                bias=st["early_less"][:], scale=1.0 / H,
            )

        def inverse_root(st):
            nc.gpsimd.tensor_tensor(out=st["rstd"][:], in0=st["var_eps"][:], in1=minus_half[:], op=ALU.pow)

        def centre(st, gain, tile, first, width):
            half, in_bank = divmod(first, BANK_CHANNELS)
            nc.vector.scalar_tensor_tensor(
                out=tile[:, first : first + width],
                in0=st["lin"][:, first : first + width],
                scalar=st["neg_mean"][:],
                in1=gain[half][:].bitcast(BF16)[:, in_bank : in_bank + width],
                op0=ALU.add,
                op1=ALU.mult,
            )

        def scale_and_shift(st, shift, tile, first, width):
            half, in_bank = divmod(first, BANK_CHANNELS)
            nc.vector.scalar_tensor_tensor(
                out=tile[:, first : first + width],
                in0=tile[:, first : first + width],
                scalar=st["rstd"][:],
                in1=shift[half][:].bitcast(BF16)[:, in_bank : in_bank + width],
                op0=ALU.mult,
                op1=ALU.add,
            )

        def diagonal_of(st):
            diagonal = stats.tile([P, P], F32)
            nc.scalar.activation(out=diagonal[:], in_=ident[:], func=ACT.Copy, scale=st["rstd"][:])
            return diagonal

        def open_with_shift(gate, t, banks):
            for half, bank in enumerate(banks):
                row = SHIFT_ROWS + gate * ROWS_PER_GATE + t * (N_TILE // ROW) + half
                nc.tensor.matmul(
                    out=bank[:, 0:ROW],
                    lhsT=ident_bf[:, row : row + 1].to_broadcast([P, P]),
                    rhs=vec_rows[:],
                    start=True,
                    stop=False,
                )

        def add_scaled(tile, diagonal, t, banks):
            for half, bank in enumerate(banks):
                first = t * N_TILE + half * ROW
                nc.tensor.matmul(
                    out=bank[:, 0:ROW], lhsT=diagonal[:], rhs=tile[:, first : first + ROW], start=False, stop=True
                )

        def squash(tile, func, first, width):
            nc.scalar.activation(out=tile[:, first : first + width], in_=tile[:, first : first + width], func=func)

        def squash_bank(tile, bank, func, t):
            nc.scalar.activation(out=tile[:, tile_cols(t)], in_=bank[:], func=func)

        def product(engine, out, in0, in1, t, op=ALU.mult):
            engine.tensor_tensor(out=out[:, tile_cols(t)], in0=in0[:, tile_cols(t)], in1=in1[:, tile_cols(t)], op=op)

        gate_i = const.tile([P, H], F32)
        gate_g = const.tile([P, H], F32)
        gate_f = const.tile([P, H], F32)
        gate_o = const.tile([P, H], F32)
        c_new = const.tile([P, H], F32)
        tanh_c = const.tile([P, H], F32)

        def whole_gate(gate, tile, func, steps, gain_before):
            acc = new_acc()
            passes(gate, acc, steps[:-gain_before])
            gain = spread_gate(GAIN_ROWS, gate)
            passes(gate, acc, steps[-gain_before:])
            shift = spread_gate(SHIFT_ROWS, gate)
            st = new_stats(gate, acc)
            for t in range(TILES):
                add_bias(st, t)
                square(st, t)
            mean(st)
            variance(st)
            inverse_root(st)
            for first in range(0, H, BANK_CHANNELS):
                centre(st, gain, tile, first, BANK_CHANNELS)
            for first in range(0, H, BANK_CHANNELS):
                scale_and_shift(st, shift, tile, first, BANK_CHANNELS)
                squash(tile, func, first, BANK_CHANNELS)

        whole_gate(GATE_I, gate_i, ACT.Sigmoid, by_pass, TILES)
        whole_gate(GATE_G, gate_g, ACT.Tanh, two_tiles_at_the_end, TILES)
        for first in range(0, H, BANK_CHANNELS):
            cols = slice(first, first + BANK_CHANNELS)
            nc.gpsimd.tensor_tensor(out=gate_i[:, cols], in0=gate_i[:, cols], in1=gate_g[:, cols], op=ALU.mult)

        acc = new_acc()
        passes(GATE_F, acc, two_tiles_at_the_end[:-TILES])
        gain = spread_gate(GAIN_ROWS, GATE_F)
        passes(GATE_F, acc, two_tiles_at_the_end[-TILES:])
        shift = spread_gate(SHIFT_ROWS, GATE_F)
        st = new_stats(GATE_F, acc)
        for t in range(TILES):
            add_bias(st, t)
            square(st, t)
        mean(st)
        variance(st)
        inverse_root(st)
        for first in range(0, H, BANK_CHANNELS):
            centre(st, gain, gate_f, first, BANK_CHANNELS)
        st_f, shift_f = st, shift
        acc = new_acc()
        passes(GATE_O, acc, tiles_at_the_end[:TILES])
        c_banks = []
        for half in range(BANKS_PER_GATE):
            bank = spread_psum.tile([P, BANK_CHANNELS], BF16, tag="bank")
            for k in range(BANK_CHANNELS // N_TILE):
                nc.tensor.matmul(
                    out=bank[:, k * N_TILE : (k + 1) * N_TILE], lhsT=ident_bf[:],
                    rhs=c_sb[:, (2 * half + k) * N_TILE : (2 * half + k + 1) * N_TILE], start=True, stop=True,
                )
            c_banks.append(bank)
        passes(GATE_O, acc, tiles_at_the_end[TILES : 2 * TILES])
        gain = [pick_rows(GAIN_ROWS, GATE_O, 0)]
        passes(GATE_O, acc, tiles_at_the_end[2 * TILES :])
        gain.append(pick_rows(GAIN_ROWS, GATE_O, 1))
        shift = [pick_rows(SHIFT_ROWS, GATE_O, 0)]
        last_banks = [
            spread_psum.tile([P, N_TILE], F32, tag="bank", name="last_bank"),
            acc_psum.tile([P, N_TILE], F32, name="acc"),
        ]
        open_with_shift(GATE_O, 3, last_banks)
        shift.append(pick_rows(SHIFT_ROWS, GATE_O, 1))
        def f_times_c(t):
            nc.vector.tensor_tensor(
                out=gate_f[:, tile_cols(t)], in0=gate_f[:, tile_cols(t)],
                in1=c_banks[t // 2][:, (t % 2) * N_TILE : (t % 2 + 1) * N_TILE], op=ALU.mult,
            )
        shift_late = work.tile([P, N_TILE], BF16)
        nc.scalar.copy(
            out=shift_late[:].bitcast(F32), in_=shift_f[1][:, N_TILE // 2 : N_TILE]
        )
        late = tile_cols(3)
        nc.scalar.activation(out=gate_f[:, late], in_=gate_f[:, late], func=ACT.Copy, scale=st_f["rstd"][:])
        nc.gpsimd.tensor_tensor(out=gate_f[:, late], in0=gate_f[:, late], in1=shift_late[:], op=ALU.add)
        for t in range(3):
            scale_and_shift(st_f, shift_f, gate_f, t * N_TILE, N_TILE)
            squash(gate_f, ACT.Sigmoid, t * N_TILE, N_TILE)
        squash(gate_f, ACT.Sigmoid, 3 * N_TILE, N_TILE)
        f_times_c(0)
        f_times_c(1)
        f_times_c(2)
        f_times_c(3)
        st = new_stats(GATE_O, acc)
        def tanh_cell(t):
            nc.scalar.activation(out=tanh_c[:, tile_cols(t)], in_=c_new[:, tile_cols(t)], func=ACT.Tanh)
            nc.sync.dma_start(out=out_1[:, tile_cols(t)], in_=c_new[:, tile_cols(t)])
        def add(engine, t):
            product(engine, c_new, gate_f, gate_i, t, ALU.add)
        def op3(t):
            scale_and_shift(st, shift, gate_o, t * N_TILE, N_TILE)
        def sig(t):
            squash(gate_o, ACT.Sigmoid, t * N_TILE, N_TILE)
        def out(first, width):
            cols = slice(first, first + width)
            nc.vector.tensor_tensor(out=gate_o[:, cols], in0=gate_o[:, cols], in1=tanh_c[:, cols], op=ALU.mult)
            nc.sync.dma_start(out=out_0[:, cols], in_=gate_o[:, cols])
        for t in range(TILES):
            add(nc.gpsimd, t)
        tanh_cell(0)
        add_bias(st, 0); square(st, 0)
        add_bias(st, 1); square(st, 1)
        add_bias(st, 2); square(st, 2)
        add_bias(st, 3); square(st, 3)
        mean(st); variance(st)
        inverse_root(st)
        for t in (0, 1, 3, 2): centre(st, gain, gate_o, t * N_TILE, N_TILE)
        tanh_cell(1)
        tanh_cell(2)
        diagonal = diagonal_of(st)
        tanh_cell(3)
        add_scaled(gate_o, diagonal, 3, last_banks)
        for t in (0, 1, 2): op3(t)
        for t in (0, 1, 2): sig(t)
        for half, bank in enumerate(last_banks):
            first = 3 * N_TILE + half * ROW
            nc.scalar.activation(out=gate_o[:, first : first + ROW], in_=bank[:, 0:ROW], func=ACT.Sigmoid)
        for t in range(TILES - 1): out(t * N_TILE, N_TILE)
        for half in range(2): out(3 * N_TILE + half * ROW, ROW)
